import numpy as np
import ml_dtypes

BF16 = ml_dtypes.bfloat16


def bf(x):
    return np.asarray(x, np.float32).astype(BF16)


def f32(x):
    return np.asarray(x, np.float32)


def f64(x):
    return np.asarray(x).astype(np.float64)


def striped(idx):
    return np.tile(idx.reshape(-1, 16).T, (8, 1))


B, L, D, H, DH, S, N, M = 4, 512, 512, 4, 128, 4096, 2048, 128
MAXF, DFMAX = 20, 10000
EPS_BN, TINY = 1e-5, 1e-12
ES, FS = 3.0, 8.0


def setup_inputs():
    emb = f32(ES * np.random.standard_normal((D, S)))
    tf = f32(np.random.permutation(np.tile(np.arange(1, MAXF + 1), N // MAXF + 1))[:N].reshape(1, N))
    df = f32(np.random.permutation(np.arange(1, DFMAX))[:N].reshape(1, N))
    bn_gamma = f32(1.0 + 0.1 * np.random.standard_normal((H, 1)))
    fc_w = bf(FS * np.random.standard_normal((D, M)) / np.sqrt(D))
    fc_b = f32(0.1 * np.random.standard_normal((M, 1)))
    return {"emb": emb, "tf": tf, "df": df, "bn_gamma": bn_gamma, "fc_w": fc_w, "fc_b": fc_b, "offs": striped(np.random.permutation(S)[:N])}


def reference(emb, tf, df, bn_gamma, fc_w, fc_b, offs):
    idx = offs[:16].T.reshape(-1)
    wt = np.log(1.0 + f64(tf)) / np.log(f64(df) + 2.0)
    h = f64(emb)[:, idx] * wt
    hh = h.reshape(H, DH, B, L)
    sq = (hh * hh).sum(axis=1)
    gram = np.einsum('hkbi,hkbu->hbiu', hh, hh)
    d2 = sq[:, :, :, None] + sq[:, :, None, :] - 2.0 * gram
    dist = np.sqrt(np.maximum(d2, 0.0) + TINY)
    mu = dist.mean(axis=(1, 2, 3), keepdims=True)
    var = ((dist - mu) ** 2).mean(axis=(1, 2, 3), keepdims=True)
    z = f64(bn_gamma).reshape(H, 1, 1, 1) * (dist - mu) / np.sqrt(var + EPS_BN)
    e = np.exp(z)
    att = e / e.sum(axis=-1, keepdims=True)
    vo = np.einsum('hbiu,hkbu->hkbi', att, hh).reshape(D, N)
    lg = f64(fc_w).T @ vo + f64(fc_b)
    ws = att.sum(axis=2).mean(axis=0).reshape(1, N)
    return np.concatenate([lg, ws], axis=0)

@@ -1,0 +1,224 @@
+import concourse.mybir as mybir
+from concourse.masks import make_identity
+
+F32 = mybir.dt.float32
+BF16 = mybir.dt.bfloat16
+U16 = mybir.dt.uint16
+ALU = mybir.AluOpType
+ACT = mybir.ActivationFunctionType
+AX = mybir.AxisListType
+
+P = 128
+HEADS, DOCS, L = 4, 4, 512
+T = L // P
+S = 4096
+N = DOCS * L
+PAIRS = DOCS * L * L
+EPS_BN, TINY = 1e-5, 1e-12
+LOWEST = -3.0e38
+KEYW = 144
+BANK = 512
+
+FLOPS = 2 * (2 * HEADS * DOCS * L * L * P) + 2 * (HEADS * P) * P * N
+BYTES = 4 * HEADS * P * N + 2 * 4 * N + 2 * N + 2 * HEADS * P * P + 4 * (P + 1) * N
+
+
+def tile_attentiontfidf_b_kernel(tc, emb, tf, df, bn_gamma, fc_w, fc_b, offs, out):
+    nc = tc.nc
+    with (
+        tc.tile_pool(name="held", bufs=1) as held,
+        tc.tile_pool(name="dists", bufs=1) as dists,
+    ):
+        offsets = held.tile([P, N // 16], U16, name="offsets")
+        nc.sync.dma_start(offsets[:], offs)
+
+        tf_c = held.tile([P, N // P], F32, name="tf_c")
+        df_c = held.tile([P, N // P], F32, name="df_c")
+        nc.scalar.dma_start(tf_c[:], tf.rearrange("o (p c) -> (o p) c", p=P))
+        nc.scalar.dma_start(df_c[:], df.rearrange("o (p c) -> (o p) c", p=P))
+        nc.vector.tensor_scalar_add(tf_c[:], tf_c[:], 1.0)
+        nc.vector.tensor_scalar_add(df_c[:], df_c[:], 2.0)
+        ln_tf = held.tile([P, N // P], F32, name="ln_tf")
+        ln_df = held.tile([P, N // P], F32, name="ln_df")
+        nc.scalar.activation(ln_tf[:], tf_c[:], ACT.Ln)
+        nc.scalar.activation(ln_df[:], df_c[:], ACT.Ln)
+        inv_ln_df = held.tile([P, N // P], F32, name="inv_ln_df")
+        nc.vector.reciprocal(inv_ln_df[:], ln_df[:])
+        wt_c = held.tile([P, N // P], F32, name="wt_c")
+        nc.vector.tensor_mul(wt_c[:], ln_tf[:], inv_ln_df[:])
+        parked = out[0:1, :]
+        nc.scalar.dma_start(parked.rearrange("o (p c) -> (o p) c", p=P), wt_c[:])
+
+        ident_bf = held.tile([P, P], BF16, name="ident_bf")
+        make_identity(nc, ident_bf[:])
+        ident_f = held.tile([P, P], F32, name="ident_f")
+        make_identity(nc, ident_f[:])
+        neg_half = held.tile([P, P], F32, name="neg_half")
+        nc.gpsimd.memset(neg_half[:], -0.5)
+        ones = held.tile([P, P], F32, name="ones")
+        nc.gpsimd.memset(ones[:], 1.0)
+        gamma = held.tile([P, HEADS], F32, name="gamma")
+        nc.gpsimd.dma_start(gamma[:], bn_gamma.rearrange("h o -> (h o)").partition_broadcast(P))
+        fcw = held.tile([P, HEADS, P], BF16, name="fcw")
+        nc.gpsimd.dma_start(fcw[:], fc_w.rearrange("(a k) m -> k a m", k=P))
+        fcb = held.tile([P, 1], F32, name="fcb")
+        nc.gpsimd.dma_start(fcb[:], fc_b)
+
+        keys = held.tile([P, HEADS * DOCS * T, KEYW], BF16, name="keys")
+        dist = [[dists.tile([P, T * L], F32, name=f"dist{a}{b}") for b in range(DOCS)] for a in range(HEADS)]
+        sum_dist = held.tile([P, HEADS * DOCS * T], F32, name="sum_dist")
+        sum_nhd = held.tile([P, HEADS * DOCS * T], F32, name="sum_nhd")
+
+        with (
+            tc.tile_pool(name="weights", bufs=1) as weights,
+            tc.tile_pool(name="tables", bufs=2) as tables,
+            tc.tile_pool(name="work", bufs=3) as work,
+            tc.tile_pool(name="halves", bufs=6) as halves,
+            tc.psum_pool(name="ps_gram", bufs=4) as ps_gram,
+            tc.psum_pool(name="ps_prep", bufs=1) as ps_prep,
+        ):
+            wt = weights.tile([P, N], F32, name="wt")
+            nc.scalar.dma_start(wt[:], parked.rearrange("o n -> (o n)").partition_broadcast(P))
+
+            for a in range(HEADS):
+                table = tables.tile([P, S], F32, name="table")
+                nc.sync.dma_start(table[:], emb[a * P:(a + 1) * P, :])
+                for b in range(DOCS):
+                    block = (a * DOCS + b) * T
+                    h = work.tile([P, L], F32, name="h")
+                    nc.vector.tensor_tensor(
+                        h[:],
+                        table[:].indirect(offsets[:, b * (L // 16):(b + 1) * (L // 16)]),
+                        wt[:, b * L:(b + 1) * L],
+                        ALU.mult,
+                    )
+                    hb = work.tile([P, L], BF16, name="hb")
+                    nc.gpsimd.tensor_copy(hb[:], h[:])
+                    hsq = work.tile([P, L], F32, name="hsq")
+                    nc.scalar.activation(hsq[:], h[:], ACT.Square)
+
+                    sqrow_ps = ps_prep.tile([P, L], F32, name="sqrow_ps")
+                    nc.tensor.matmul(sqrow_ps[:], neg_half[:], hsq[:], start=True, stop=True)
+                    sqrow = work.tile([P, L], F32, name="sqrow")
+                    nc.scalar.activation(sqrow[:], sqrow_ps[:], ACT.Copy)
+                    sqcol_ps = ps_prep.tile([P, T], F32, name="sqcol_ps")
+                    for t in range(T):
+                        nc.tensor.matmul(
+                            sqcol_ps[:, t:t + 1], hsq[:, t * P:(t + 1) * P], neg_half[:, 0:1], start=True, stop=True
+                        )
+                    sqcol = work.tile([P, T], F32, name="sqcol")
+                    nc.vector.tensor_scalar_add(sqcol[:], sqcol_ps[:], -0.5 * TINY)
+
+                    hT_ps = ps_prep.tile([P, T, P], BF16, name="hT_ps")
+                    for t in range(T):
+                        nc.tensor.transpose(hT_ps[:, t, :], hb[:, t * P:(t + 1) * P], ident_bf[:])
+                    nc.vector.tensor_copy(keys[:, block:block + T, 0:P], hT_ps[:])
+
+                    for t in range(T):
+                        gram_ps = ps_gram.tile([P, L], F32, name="gram_ps")
+                        nc.tensor.matmul(gram_ps[:], hb[:, t * P:(t + 1) * P], hb[:], start=True, stop=True)
+                        nhd = halves.tile([P, L], F32, name="nhd")
+                        nc.vector.scalar_tensor_tensor(
+                            nhd[:], gram_ps[:], sqcol[:, t:t + 1], sqrow[:], ALU.add, ALU.add,
+                            accum_out=sum_nhd[:, block + t:block + t + 1],
+                        )
+                        nc.gpsimd.tensor_scalar(nhd[:], nhd[:], -0.5 * TINY, LOWEST, ALU.min, ALU.max)
+                        nc.scalar.activation(
+                            dist[a][b][:, t * L:(t + 1) * L], nhd[:], ACT.Sqrt, scale=-2.0,
+                            accum_out=sum_dist[:, block + t:block + t + 1],
+                        )
+
+        gain = held.tile([P, HEADS], F32, name="gain")
+        shift = held.tile([P, HEADS], F32, name="shift")
+        with tc.psum_pool(name="ps_stat", bufs=1) as ps_stat:
+            sums = held.tile([P, 2 * HEADS], F32, name="sums")
+            nc.vector.tensor_reduce(
+                sums[:, 0:HEADS], sum_dist[:].rearrange("p (a c) -> p a c", a=HEADS), AX.X, ALU.add
+            )
+            nc.vector.tensor_reduce(
+                sums[:, HEADS:2 * HEADS], sum_nhd[:].rearrange("p (a c) -> p a c", a=HEADS), AX.X, ALU.add
+            )
+            total_ps = ps_stat.tile([P, 2 * HEADS], F32, name="total_ps")
+            nc.tensor.matmul(total_ps[:], ones[:], sums[:], start=True, stop=True)
+            mean = held.tile([P, HEADS], F32, name="mean")
+            nc.vector.tensor_scalar_mul(mean[:], total_ps[:, 0:HEADS], 1.0 / PAIRS)
+            mean_sq = held.tile([P, HEADS], F32, name="mean_sq")
+            nc.vector.tensor_scalar_mul(mean_sq[:], total_ps[:, HEADS:2 * HEADS], -2.0 / PAIRS)
+            sq_mean = held.tile([P, HEADS], F32, name="sq_mean")
+            nc.vector.tensor_mul(sq_mean[:], mean[:], mean[:])
+            var_eps = held.tile([P, HEADS], F32, name="var_eps")
+            nc.vector.scalar_tensor_tensor(var_eps[:], mean_sq[:], EPS_BN, sq_mean[:], ALU.add, ALU.subtract)
+            sd = held.tile([P, HEADS], F32, name="sd")
+            nc.scalar.activation(sd[:], var_eps[:], ACT.Sqrt)
+            inv_sd = held.tile([P, HEADS], F32, name="inv_sd")
+            nc.vector.reciprocal(inv_sd[:], sd[:])
+            nc.vector.tensor_mul(gain[:], gamma[:], inv_sd[:])
+            nc.vector.scalar_tensor_tensor(shift[:], mean[:], -1.0, gain[:], ALU.mult, ALU.mult)
+
+        received = held.tile([P, HEADS * DOCS * T], F32, name="received")
+        with (
+            tc.tile_pool(name="exps", bufs=12) as exps,
+            tc.tile_pool(name="small", bufs=3) as small,
+            tc.tile_pool(name="vos", bufs=2 * HEADS) as vos,
+            tc.tile_pool(name="outs", bufs=2) as outs,
+            tc.psum_pool(name="ps_v", bufs=3) as ps_v,
+            tc.psum_pool(name="ps_t", bufs=2) as ps_t,
+            tc.psum_pool(name="ps_o", bufs=1) as ps_o,
+        ):
+            for b in range(DOCS):
+                vo = []
+                for a in range(HEADS):
+                    block = (a * DOCS + b) * T
+                    rowsum = small.tile([P, T], F32, name="rowsum")
+                    e = []
+                    for t in range(T):
+                        e_t = exps.tile([P, L], BF16, name="e_t")
+                        nc.scalar.activation(
+                            e_t[:], dist[a][b][:, t * L:(t + 1) * L], ACT.Exp,
+                            bias=shift[:, a:a + 1], scale=gain[:, a:a + 1], accum_out=rowsum[:, t:t + 1],
+                        )
+                        e.append(e_t)
+                    rinv = small.tile([P, T], F32, name="rinv")
+                    nc.vector.reciprocal(rinv[:], rowsum[:])
+                    nc.vector.tensor_copy(keys[:, block:block + T, P:P + 1].squeeze(2), rinv[:])
+
+                    voT = small.tile([P, T, P], BF16, name="voT")
+                    for pair in range(T // 2):
+                        v_ps = ps_v.tile([P, 2, BANK // 2], F32, name="v_ps")
+                        for g in range(2):
+                            s = 2 * pair + g
+                            for t in range(T):
+                                nc.tensor.matmul(
+                                    v_ps[:, g, 0:P + 1], e[t][:, s * P:(s + 1) * P], keys[:, block + t, 0:P + 1],
+                                    start=(t == 0), stop=(t == T - 1),
+                                )
+                        nc.vector.tensor_tensor(
+                            voT[:, 2 * pair:2 * pair + 2, :], v_ps[:, :, 0:P],
+                            rinv[:, 2 * pair:2 * pair + 2].unsqueeze(2).to_broadcast([P, 2, P]), ALU.mult,
+                        )
+                        nc.vector.tensor_copy(
+                            received[:, block + 2 * pair:block + 2 * pair + 2], v_ps[:, :, P:P + 1].squeeze(2)
+                        )
+                    vo_ps = ps_t.tile([P, L], BF16, name="vo_ps")
+                    for s in range(T):
+                        nc.tensor.transpose(vo_ps[:, s * P:(s + 1) * P], voT[:, s, :], ident_bf[:])
+                    vo_a = vos.tile([P, L], BF16, name="vo_a")
+                    nc.vector.tensor_copy(vo_a[:], vo_ps[:])
+                    vo.append(vo_a)
+
+                lg_ps = ps_o.tile([P, L], F32, name="lg_ps")
+                for a in range(HEADS):
+                    nc.tensor.matmul(lg_ps[:], fcw[:, a, :], vo[a][:], start=(a == 0), stop=(a == HEADS - 1))
+                lg = outs.tile([P, L], F32, name="lg")
+                nc.vector.tensor_scalar_add(lg[:], lg_ps[:], fcb[:, 0:1])
+                nc.sync.dma_start(out[0:P, b * L:(b + 1) * L], lg[:])
+
+            received_sum = small.tile([P, DOCS * T], F32, name="received_sum")
+            nc.vector.tensor_reduce(
+                received_sum[:], received[:].rearrange("p (a c) -> p c a", a=HEADS), AX.X, ALU.add
+            )
+            ws_ps = ps_o.tile([P, P], F32, name="ws_ps")
+            nc.tensor.transpose(ws_ps[0:DOCS * T, :], received_sum[:], ident_f[:])
+            ws = outs.tile([DOCS * T, P], F32, name="ws")
+            nc.vector.tensor_scalar_mul(ws[:], ws_ps[0:DOCS * T, :], 1.0 / HEADS)
+            nc.sync.dma_start(out[P:P + 1, :].rearrange("o (c p) -> (o c) p", p=P), ws[:])

@@ -15,7 +15,6 @@ S = 4096
 N = DOCS * L
 PAIRS = DOCS * L * L
 EPS_BN, TINY = 1e-5, 1e-12
-LOWEST = -3.0e38
 KEYW = 144
 BANK = 512
 
@@ -66,14 +65,13 @@ def tile_attentiontfidf_b_kernel(tc, emb, tf, df, bn_gamma, fc_w, fc_b, offs, ou
 
         keys = held.tile([P, HEADS * DOCS * T, KEYW], BF16, name="keys")
         dist = [[dists.tile([P, T * L], F32, name=f"dist{a}{b}") for b in range(DOCS)] for a in range(HEADS)]
-        sum_dist = held.tile([P, HEADS * DOCS * T], F32, name="sum_dist")
+        sum_dist = held.tile([P, HEADS * DOCS], F32, name="sum_dist")
         sum_nhd = held.tile([P, HEADS * DOCS * T], F32, name="sum_nhd")
 
         with (
             tc.tile_pool(name="weights", bufs=1) as weights,
             tc.tile_pool(name="tables", bufs=2) as tables,
             tc.tile_pool(name="work", bufs=3) as work,
-            tc.tile_pool(name="halves", bufs=6) as halves,
             tc.psum_pool(name="ps_gram", bufs=4) as ps_gram,
             tc.psum_pool(name="ps_prep", bufs=1) as ps_prep,
         ):
@@ -112,21 +110,20 @@ def tile_attentiontfidf_b_kernel(tc, emb, tf, df, bn_gamma, fc_w, fc_b, offs, ou
                     hT_ps = ps_prep.tile([P, T, P], BF16, name="hT_ps")
                     for t in range(T):
                         nc.tensor.transpose(hT_ps[:, t, :], hb[:, t * P:(t + 1) * P], ident_bf[:])
-                    nc.vector.tensor_copy(keys[:, block:block + T, 0:P], hT_ps[:])
+                    nc.scalar.activation(keys[:, block:block + T, 0:P], hT_ps[:], ACT.Copy)
 
                     for t in range(T):
                         gram_ps = ps_gram.tile([P, L], F32, name="gram_ps")
                         nc.tensor.matmul(gram_ps[:], hb[:, t * P:(t + 1) * P], hb[:], start=True, stop=True)
-                        nhd = halves.tile([P, L], F32, name="nhd")
                         nc.vector.scalar_tensor_tensor(
-                            nhd[:], gram_ps[:], sqcol[:, t:t + 1], sqrow[:], ALU.add, ALU.add,
+                            dist[a][b][:, t * L:(t + 1) * L], gram_ps[:], sqcol[:, t:t + 1], sqrow[:], ALU.add, ALU.add,
                             accum_out=sum_nhd[:, block + t:block + t + 1],
                         )
-                        nc.gpsimd.tensor_scalar(nhd[:], nhd[:], -0.5 * TINY, LOWEST, ALU.min, ALU.max)
-                        nc.scalar.activation(
-                            dist[a][b][:, t * L:(t + 1) * L], nhd[:], ACT.Sqrt, scale=-2.0,
-                            accum_out=sum_dist[:, block + t:block + t + 1],
-                        )
+                    nc.vector.tensor_scalar_min(dist[a][b][:], dist[a][b][:], -0.5 * TINY)
+                    nc.scalar.activation(
+                        dist[a][b][:], dist[a][b][:], ACT.Sqrt, scale=-2.0,
+                        accum_out=sum_dist[:, a * DOCS + b:a * DOCS + b + 1],
+                    )
 
         gain = held.tile([P, HEADS], F32, name="gain")
         shift = held.tile([P, HEADS], F32, name="shift")

@@ -15,6 +15,7 @@ S = 4096
 N = DOCS * L
 PAIRS = DOCS * L * L
 EPS_BN, TINY = 1e-5, 1e-12
+LOWEST = -3.0e38
 KEYW = 144
 BANK = 512
 
@@ -56,6 +57,8 @@ def tile_attentiontfidf_b_kernel(tc, emb, tf, df, bn_gamma, fc_w, fc_b, offs, ou
         nc.gpsimd.memset(neg_half[:], -0.5)
         ones = held.tile([P, P], F32, name="ones")
         nc.gpsimd.memset(ones[:], 1.0)
+        one_bf = held.tile([P, 1], BF16, name="one_bf")
+        nc.gpsimd.memset(one_bf[:], 1.0)
         gamma = held.tile([P, HEADS], F32, name="gamma")
         nc.gpsimd.dma_start(gamma[:], bn_gamma.rearrange("h o -> (h o)").partition_broadcast(P))
         fcw = held.tile([P, HEADS, P], BF16, name="fcw")
@@ -66,7 +69,8 @@ def tile_attentiontfidf_b_kernel(tc, emb, tf, df, bn_gamma, fc_w, fc_b, offs, ou
         keys = held.tile([P, HEADS * DOCS * T, KEYW], BF16, name="keys")
         dist = [[dists.tile([P, T * L], F32, name=f"dist{a}{b}") for b in range(DOCS)] for a in range(HEADS)]
         sum_dist = held.tile([P, HEADS * DOCS], F32, name="sum_dist")
-        sum_nhd = held.tile([P, HEADS * DOCS * T], F32, name="sum_nhd")
+        sqcol = held.tile([P, HEADS * DOCS * T], F32, name="sqcol")
+        hsum_sq = held.tile([P, HEADS * DOCS], F32, name="hsum_sq")
 
         with (
             tc.tile_pool(name="weights", bufs=1) as weights,
@@ -75,6 +79,7 @@ def tile_attentiontfidf_b_kernel(tc, emb, tf, df, bn_gamma, fc_w, fc_b, offs, ou
             tc.psum_pool(name="ps_gram", bufs=4) as ps_gram,
             tc.psum_pool(name="ps_prep", bufs=1) as ps_prep,
         ):
+            hsum_ps = ps_prep.tile([P, HEADS * DOCS], F32, name="hsum_ps")
             wt = weights.tile([P, N], F32, name="wt")
             nc.scalar.dma_start(wt[:], parked.rearrange("o n -> (o n)").partition_broadcast(P))
 
@@ -104,26 +109,32 @@ def tile_attentiontfidf_b_kernel(tc, emb, tf, df, bn_gamma, fc_w, fc_b, offs, ou
                         nc.tensor.matmul(
                             sqcol_ps[:, t:t + 1], hsq[:, t * P:(t + 1) * P], neg_half[:, 0:1], start=True, stop=True
                         )
-                    sqcol = work.tile([P, T], F32, name="sqcol")
-                    nc.vector.tensor_scalar_add(sqcol[:], sqcol_ps[:], -0.5 * TINY)
+                    nc.vector.tensor_scalar_add(sqcol[:, block:block + T], sqcol_ps[:], -0.5 * TINY)
 
                     hT_ps = ps_prep.tile([P, T, P], BF16, name="hT_ps")
                     for t in range(T):
                         nc.tensor.transpose(hT_ps[:, t, :], hb[:, t * P:(t + 1) * P], ident_bf[:])
                     nc.scalar.activation(keys[:, block:block + T, 0:P], hT_ps[:], ACT.Copy)
+                    for t in range(T):
+                        nc.tensor.matmul(
+                            hsum_ps[:, a * DOCS + b:a * DOCS + b + 1], keys[:, block + t, 0:P], one_bf[:],
+                            start=(t == 0), stop=(t == T - 1),
+                        )
 
                     for t in range(T):
                         gram_ps = ps_gram.tile([P, L], F32, name="gram_ps")
                         nc.tensor.matmul(gram_ps[:], hb[:, t * P:(t + 1) * P], hb[:], start=True, stop=True)
                         nc.vector.scalar_tensor_tensor(
-                            dist[a][b][:, t * L:(t + 1) * L], gram_ps[:], sqcol[:, t:t + 1], sqrow[:], ALU.add, ALU.add,
-                            accum_out=sum_nhd[:, block + t:block + t + 1],
+                            dist[a][b][:, t * L:(t + 1) * L], gram_ps[:], sqcol[:, block + t:block + t + 1], sqrow[:],
+                            ALU.add, ALU.add,
                         )
-                    nc.vector.tensor_scalar_min(dist[a][b][:], dist[a][b][:], -0.5 * TINY)
+                    clamper = nc.gpsimd if b % 2 == 0 else nc.vector
+                    clamper.tensor_scalar(dist[a][b][:], dist[a][b][:], -0.5 * TINY, LOWEST, ALU.min, ALU.max)
                     nc.scalar.activation(
                         dist[a][b][:], dist[a][b][:], ACT.Sqrt, scale=-2.0,
                         accum_out=sum_dist[:, a * DOCS + b:a * DOCS + b + 1],
                     )
+            nc.scalar.activation(hsum_sq[:], hsum_ps[:], ACT.Square)
 
         gain = held.tile([P, HEADS], F32, name="gain")
         shift = held.tile([P, HEADS], F32, name="shift")
@@ -132,8 +143,12 @@ def tile_attentiontfidf_b_kernel(tc, emb, tf, df, bn_gamma, fc_w, fc_b, offs, ou
             nc.vector.tensor_reduce(
                 sums[:, 0:HEADS], sum_dist[:].rearrange("p (a c) -> p a c", a=HEADS), AX.X, ALU.add
             )
-            nc.vector.tensor_reduce(
-                sums[:, HEADS:2 * HEADS], sum_nhd[:].rearrange("p (a c) -> p a c", a=HEADS), AX.X, ALU.add
+            sum_hsum_sq = held.tile([P, HEADS], F32, name="sum_hsum_sq")
+            nc.vector.tensor_reduce(sum_hsum_sq[:], hsum_sq[:].rearrange("p (a c) -> p a c", a=HEADS), AX.X, ALU.add)
+            sum_sqcol = held.tile([P, HEADS], F32, name="sum_sqcol")
+            nc.vector.tensor_reduce(sum_sqcol[:], sqcol[:].rearrange("p (a c) -> p a c", a=HEADS), AX.X, ALU.add)
+            nc.vector.scalar_tensor_tensor(
+                sums[:, HEADS:2 * HEADS], sum_sqcol[:], 2.0 * L, sum_hsum_sq[:], ALU.mult, ALU.add
             )
             total_ps = ps_stat.tile([P, 2 * HEADS], F32, name="total_ps")
             nc.tensor.matmul(total_ps[:], ones[:], sums[:], start=True, stop=True)

@@ -98,7 +98,7 @@ def tile_attentiontfidf_b_kernel(tc, emb, tf, df, bn_gamma, fc_w, fc_b, offs, ou
                     hb = work.tile([P, L], BF16, name="hb")
                     nc.gpsimd.tensor_copy(hb[:], h[:])
                     hsq = work.tile([P, L], F32, name="hsq")
-                    nc.scalar.activation(hsq[:], h[:], ACT.Square)
+                    nc.gpsimd.tensor_mul(hsq[:], h[:], h[:])
 
                     sqrow_ps = ps_prep.tile([P, L], F32, name="sqrow_ps")
                     nc.tensor.matmul(sqrow_ps[:], neg_half[:], hsq[:], start=True, stop=True)

@@ -15,9 +15,15 @@ S = 4096
 N = DOCS * L
 PAIRS = DOCS * L * L
 EPS_BN, TINY = 1e-5, 1e-12
-LOWEST = -3.0e38
 KEYW = 144
 BANK = 512
+
+FIRST = [t * P for t in range(T)]
+WIDTH = [L - first for first in FIRST]
+START = [sum(WIDTH[:t]) for t in range(T)]
+KEPT = sum(WIDTH)
+BELOW = [sum(FIRST[:t]) for t in range(T)]
+MIRRORED = sum(FIRST)
 
 FLOPS = 2 * (2 * HEADS * DOCS * L * L * P) + 2 * (HEADS * P) * P * N
 BYTES = 4 * HEADS * P * N + 2 * 4 * N + 2 * N + 2 * HEADS * P * P + 4 * (P + 1) * N
@@ -29,19 +35,16 @@ def tile_attentiontfidf_b_kernel(tc, emb, tf, df, bn_gamma, fc_w, fc_b, offs, ou
         tc.tile_pool(name="held", bufs=1) as held,
         tc.tile_pool(name="dists", bufs=1) as dists,
     ):
-        offsets = held.tile([P, N // 16], U16, name="offsets")
-        nc.sync.dma_start(offsets[:], offs)
-
         tf_c = held.tile([P, N // P], F32, name="tf_c")
         df_c = held.tile([P, N // P], F32, name="df_c")
-        nc.scalar.dma_start(tf_c[:], tf.rearrange("o (p c) -> (o p) c", p=P))
+        nc.sync.dma_start(tf_c[:], tf.rearrange("o (p c) -> (o p) c", p=P))
         nc.scalar.dma_start(df_c[:], df.rearrange("o (p c) -> (o p) c", p=P))
-        nc.vector.tensor_scalar_add(tf_c[:], tf_c[:], 1.0)
-        nc.vector.tensor_scalar_add(df_c[:], df_c[:], 2.0)
+        offsets = held.tile([P, N // 16], U16, name="offsets")
+        nc.sync.dma_start(offsets[:], offs)
         ln_tf = held.tile([P, N // P], F32, name="ln_tf")
         ln_df = held.tile([P, N // P], F32, name="ln_df")
-        nc.scalar.activation(ln_tf[:], tf_c[:], ACT.Ln)
-        nc.scalar.activation(ln_df[:], df_c[:], ACT.Ln)
+        nc.scalar.activation(ln_tf[:], tf_c[:], ACT.Ln, bias=1.0)
+        nc.scalar.activation(ln_df[:], df_c[:], ACT.Ln, bias=2.0)
         inv_ln_df = held.tile([P, N // P], F32, name="inv_ln_df")
         nc.vector.reciprocal(inv_ln_df[:], ln_df[:])
         wt_c = held.tile([P, N // P], F32, name="wt_c")
@@ -67,8 +70,10 @@ def tile_attentiontfidf_b_kernel(tc, emb, tf, df, bn_gamma, fc_w, fc_b, offs, ou
         nc.gpsimd.dma_start(fcb[:], fc_b)
 
         keys = held.tile([P, HEADS * DOCS * T, KEYW], BF16, name="keys")
-        dist = [[dists.tile([P, T * L], F32, name=f"dist{a}{b}") for b in range(DOCS)] for a in range(HEADS)]
-        sum_dist = held.tile([P, HEADS * DOCS], F32, name="sum_dist")
+        dist = [[dists.tile([P, KEPT], F32, name=f"dist{a}{b}") for b in range(DOCS)] for a in range(HEADS)]
+        sum_once = held.tile([P, HEADS * DOCS * T], F32, name="sum_once")
+        sum_twice = held.tile([P, HEADS * DOCS * T], F32, name="sum_twice")
+        nc.gpsimd.memset(sum_twice[:], 0.0)
         sqcol = held.tile([P, HEADS * DOCS * T], F32, name="sqcol")
         hsum_sq = held.tile([P, HEADS * DOCS], F32, name="hsum_sq")
 
@@ -80,8 +85,11 @@ def tile_attentiontfidf_b_kernel(tc, emb, tf, df, bn_gamma, fc_w, fc_b, offs, ou
             tc.psum_pool(name="ps_prep", bufs=1) as ps_prep,
         ):
             hsum_ps = ps_prep.tile([P, HEADS * DOCS], F32, name="hsum_ps")
-            wt = weights.tile([P, N], F32, name="wt")
-            nc.scalar.dma_start(wt[:], parked.rearrange("o n -> (o n)").partition_broadcast(P))
+            wt = [weights.tile([P, L], F32, name=f"wt{b}") for b in range(DOCS)]
+            for b in range(DOCS):
+                nc.scalar.dma_start(
+                    wt[b][:], parked[:, b * L:(b + 1) * L].rearrange("o n -> (o n)").partition_broadcast(P)
+                )
 
             for a in range(HEADS):
                 table = tables.tile([P, S], F32, name="table")
@@ -92,13 +100,13 @@ def tile_attentiontfidf_b_kernel(tc, emb, tf, df, bn_gamma, fc_w, fc_b, offs, ou
                     nc.vector.tensor_tensor(
                         h[:],
                         table[:].indirect(offsets[:, b * (L // 16):(b + 1) * (L // 16)]),
-                        wt[:, b * L:(b + 1) * L],
+                        wt[b][:],
                         ALU.mult,
                     )
                     hb = work.tile([P, L], BF16, name="hb")
                     nc.gpsimd.tensor_copy(hb[:], h[:])
                     hsq = work.tile([P, L], F32, name="hsq")
-                    nc.gpsimd.tensor_mul(hsq[:], h[:], h[:])
+                    nc.scalar.activation(hsq[:], h[:], ACT.Square)
 
                     sqrow_ps = ps_prep.tile([P, L], F32, name="sqrow_ps")
                     nc.tensor.matmul(sqrow_ps[:], neg_half[:], hsq[:], start=True, stop=True)
@@ -109,7 +117,7 @@ def tile_attentiontfidf_b_kernel(tc, emb, tf, df, bn_gamma, fc_w, fc_b, offs, ou
                         nc.tensor.matmul(
                             sqcol_ps[:, t:t + 1], hsq[:, t * P:(t + 1) * P], neg_half[:, 0:1], start=True, stop=True
                         )
-                    nc.vector.tensor_scalar_add(sqcol[:, block:block + T], sqcol_ps[:], -0.5 * TINY)
+                    nc.scalar.activation(sqcol[:, block:block + T], sqcol_ps[:], ACT.Identity, bias=-0.5 * TINY)
 
                     hT_ps = ps_prep.tile([P, T, P], BF16, name="hT_ps")
                     for t in range(T):
@@ -123,26 +131,35 @@ def tile_attentiontfidf_b_kernel(tc, emb, tf, df, bn_gamma, fc_w, fc_b, offs, ou
 
                     for t in range(T):
                         gram_ps = ps_gram.tile([P, L], F32, name="gram_ps")
-                        nc.tensor.matmul(gram_ps[:], hb[:, t * P:(t + 1) * P], hb[:], start=True, stop=True)
-                        nc.vector.scalar_tensor_tensor(
-                            dist[a][b][:, t * L:(t + 1) * L], gram_ps[:], sqcol[:, block + t:block + t + 1], sqrow[:],
-                            ALU.add, ALU.add,
+                        nc.tensor.matmul(
+                            gram_ps[:, 0:WIDTH[t]], hb[:, t * P:(t + 1) * P], hb[:, FIRST[t]:L], start=True, stop=True
                         )
-                    clamper = nc.gpsimd if b % 2 == 0 else nc.vector
-                    clamper.tensor_scalar(dist[a][b][:], dist[a][b][:], -0.5 * TINY, LOWEST, ALU.min, ALU.max)
-                    nc.scalar.activation(
-                        dist[a][b][:], dist[a][b][:], ACT.Sqrt, scale=-2.0,
-                        accum_out=sum_dist[:, a * DOCS + b:a * DOCS + b + 1],
-                    )
+                        nc.vector.scalar_tensor_tensor(
+                            dist[a][b][:, START[t]:START[t] + WIDTH[t]], gram_ps[:, 0:WIDTH[t]],
+                            sqcol[:, block + t:block + t + 1], sqrow[:, FIRST[t]:L], ALU.add, ALU.add,
+                        )
+                    nc.vector.tensor_scalar_min(dist[a][b][:], dist[a][b][:], -0.5 * TINY)
+                    for t in range(T):
+                        diagonal = dist[a][b][:, START[t]:START[t] + P]
+                        nc.scalar.activation(
+                            diagonal, diagonal, ACT.Sqrt, scale=-2.0, accum_out=sum_once[:, block + t:block + t + 1]
+                        )
+                        if WIDTH[t] > P:
+                            right = dist[a][b][:, START[t] + P:START[t] + WIDTH[t]]
+                            nc.scalar.activation(
+                                right, right, ACT.Sqrt, scale=-2.0, accum_out=sum_twice[:, block + t:block + t + 1]
+                            )
             nc.scalar.activation(hsum_sq[:], hsum_ps[:], ACT.Square)
 
         gain = held.tile([P, HEADS], F32, name="gain")
         shift = held.tile([P, HEADS], F32, name="shift")
         with tc.psum_pool(name="ps_stat", bufs=1) as ps_stat:
             sums = held.tile([P, 2 * HEADS], F32, name="sums")
-            nc.vector.tensor_reduce(
-                sums[:, 0:HEADS], sum_dist[:].rearrange("p (a c) -> p a c", a=HEADS), AX.X, ALU.add
-            )
+            once = held.tile([P, HEADS], F32, name="once")
+            nc.vector.tensor_reduce(once[:], sum_once[:].rearrange("p (a c) -> p a c", a=HEADS), AX.X, ALU.add)
+            twice = held.tile([P, HEADS], F32, name="twice")
+            nc.vector.tensor_reduce(twice[:], sum_twice[:].rearrange("p (a c) -> p a c", a=HEADS), AX.X, ALU.add)
+            nc.vector.scalar_tensor_tensor(sums[:, 0:HEADS], twice[:], 2.0, once[:], ALU.mult, ALU.add)
             sum_hsum_sq = held.tile([P, HEADS], F32, name="sum_hsum_sq")
             nc.vector.tensor_reduce(sum_hsum_sq[:], hsum_sq[:].rearrange("p (a c) -> p a c", a=HEADS), AX.X, ALU.add)
             sum_sqcol = held.tile([P, HEADS], F32, name="sum_sqcol")
@@ -169,29 +186,41 @@ def tile_attentiontfidf_b_kernel(tc, emb, tf, df, bn_gamma, fc_w, fc_b, offs, ou
 
         received = held.tile([P, HEADS * DOCS * T], F32, name="received")
         with (
-            tc.tile_pool(name="exps", bufs=12) as exps,
+            tc.tile_pool(name="exps", bufs=3) as exps,
             tc.tile_pool(name="small", bufs=3) as small,
             tc.tile_pool(name="vos", bufs=2 * HEADS) as vos,
             tc.tile_pool(name="outs", bufs=2) as outs,
             tc.psum_pool(name="ps_v", bufs=3) as ps_v,
             tc.psum_pool(name="ps_t", bufs=2) as ps_t,
             tc.psum_pool(name="ps_o", bufs=1) as ps_o,
+            tc.psum_pool(name="ps_e", bufs=2) as ps_e,
         ):
             for b in range(DOCS):
                 vo = []
                 for a in range(HEADS):
                     block = (a * DOCS + b) * T
-                    rowsum = small.tile([P, T], F32, name="rowsum")
-                    e = []
+                    e = exps.tile([P, T, L], BF16, name="e")
+                    right_sum = small.tile([P, T], F32, name="right_sum")
                     for t in range(T):
-                        e_t = exps.tile([P, L], BF16, name="e_t")
                         nc.scalar.activation(
-                            e_t[:], dist[a][b][:, t * L:(t + 1) * L], ACT.Exp,
-                            bias=shift[:, a:a + 1], scale=gain[:, a:a + 1], accum_out=rowsum[:, t:t + 1],
+                            e[:, t, FIRST[t]:L], dist[a][b][:, START[t]:START[t] + WIDTH[t]], ACT.Exp,
+                            bias=shift[:, a:a + 1], scale=gain[:, a:a + 1], accum_out=right_sum[:, t:t + 1],
                         )
-                        e.append(e_t)
+                    eT_ps = ps_e.tile([P, MIRRORED], BF16, name="eT_ps")
+                    rowsum = small.tile([P, T], F32, name="rowsum")
+                    for t in range(1, T):
+                        for s in range(t):
+                            nc.tensor.transpose(
+                                eT_ps[:, BELOW[t] + s * P:BELOW[t] + (s + 1) * P], e[:, s, t * P:(t + 1) * P], ident_bf[:]
+                            )
+                    for t in range(1, T):
+                        nc.vector.tensor_scalar(
+                            e[:, t, 0:FIRST[t]], eT_ps[:, BELOW[t]:BELOW[t] + FIRST[t]], 1.0, right_sum[:, t:t + 1],
+                            ALU.mult, ALU.add, accum_out=rowsum[:, t:t + 1],
+                        )
                     rinv = small.tile([P, T], F32, name="rinv")
-                    nc.vector.reciprocal(rinv[:], rowsum[:])
+                    nc.vector.reciprocal(rinv[:, 0:1], right_sum[:, 0:1])
+                    nc.vector.reciprocal(rinv[:, 1:T], rowsum[:, 1:T])
                     nc.vector.tensor_copy(keys[:, block:block + T, P:P + 1].squeeze(2), rinv[:])
 
                     voT = small.tile([P, T, P], BF16, name="voT")
@@ -201,7 +230,7 @@ def tile_attentiontfidf_b_kernel(tc, emb, tf, df, bn_gamma, fc_w, fc_b, offs, ou
                             s = 2 * pair + g
                             for t in range(T):
                                 nc.tensor.matmul(
-                                    v_ps[:, g, 0:P + 1], e[t][:, s * P:(s + 1) * P], keys[:, block + t, 0:P + 1],
+                                    v_ps[:, g, 0:P + 1], e[:, t, s * P:(s + 1) * P], keys[:, block + t, 0:P + 1],
                                     start=(t == 0), stop=(t == T - 1),
                                 )
                         nc.vector.tensor_tensor(
@@ -215,7 +244,7 @@ def tile_attentiontfidf_b_kernel(tc, emb, tf, df, bn_gamma, fc_w, fc_b, offs, ou
                     for s in range(T):
                         nc.tensor.transpose(vo_ps[:, s * P:(s + 1) * P], voT[:, s, :], ident_bf[:])
                     vo_a = vos.tile([P, L], BF16, name="vo_a")
-                    nc.vector.tensor_copy(vo_a[:], vo_ps[:])
+                    nc.scalar.activation(vo_a[:], vo_ps[:], ACT.Copy)
                     vo.append(vo_a)
 
                 lg_ps = ps_o.tile([P, L], F32, name="lg_ps")
@@ -229,7 +258,7 @@ def tile_attentiontfidf_b_kernel(tc, emb, tf, df, bn_gamma, fc_w, fc_b, offs, ou
             nc.vector.tensor_reduce(
                 received_sum[:], received[:].rearrange("p (a c) -> p c a", a=HEADS), AX.X, ALU.add
             )
-            ws_ps = ps_o.tile([P, P], F32, name="ws_ps")
+            ws_ps = ps_o.tile([P, P], F32, name="ws_ps", tag="lg_ps")
             nc.tensor.transpose(ws_ps[0:DOCS * T, :], received_sum[:], ident_f[:])
             ws = outs.tile([DOCS * T, P], F32, name="ws")
             nc.vector.tensor_scalar_mul(ws[:], ws_ps[0:DOCS * T, :], 1.0 / HEADS)

@@ -13,6 +13,8 @@ HEADS, DOCS, L = 4, 4, 512
 T = L // P
 S = 4096
 N = DOCS * L
+C = N // P
+TABLE_BYTES = 4 * S
 PAIRS = DOCS * L * L
 EPS_BN, TINY = 1e-5, 1e-12
 KEYW = 144
@@ -35,120 +37,140 @@ def tile_attentiontfidf_b_kernel(tc, emb, tf, df, bn_gamma, fc_w, fc_b, offs, ou
         tc.tile_pool(name="held", bufs=1) as held,
         tc.tile_pool(name="dists", bufs=1) as dists,
     ):
-        tf_c = held.tile([P, N // P], F32, name="tf_c")
-        df_c = held.tile([P, N // P], F32, name="df_c")
+        tf_c = held.tile([P, C], F32, name="tf_c")
+        df_c = held.tile([P, C], F32, name="df_c")
         nc.sync.dma_start(tf_c[:], tf.rearrange("o (p c) -> (o p) c", p=P))
         nc.scalar.dma_start(df_c[:], df.rearrange("o (p c) -> (o p) c", p=P))
         offsets = held.tile([P, N // 16], U16, name="offsets")
         nc.sync.dma_start(offsets[:], offs)
-        ln_tf = held.tile([P, N // P], F32, name="ln_tf")
-        ln_df = held.tile([P, N // P], F32, name="ln_df")
-        nc.scalar.activation(ln_tf[:], tf_c[:], ACT.Ln, bias=1.0)
-        nc.scalar.activation(ln_df[:], df_c[:], ACT.Ln, bias=2.0)
-        inv_ln_df = held.tile([P, N // P], F32, name="inv_ln_df")
-        nc.vector.reciprocal(inv_ln_df[:], ln_df[:])
-        wt_c = held.tile([P, N // P], F32, name="wt_c")
-        nc.vector.tensor_mul(wt_c[:], ln_tf[:], inv_ln_df[:])
-        parked = out[0:1, :]
-        nc.scalar.dma_start(parked.rearrange("o (p c) -> (o p) c", p=P), wt_c[:])
 
-        ident_bf = held.tile([P, P], BF16, name="ident_bf")
-        make_identity(nc, ident_bf[:])
         ident_f = held.tile([P, P], F32, name="ident_f")
         make_identity(nc, ident_f[:])
-        neg_half = held.tile([P, P], F32, name="neg_half")
-        nc.gpsimd.memset(neg_half[:], -0.5)
         ones = held.tile([P, P], F32, name="ones")
-        nc.gpsimd.memset(ones[:], 1.0)
+        nc.vector.memset(ones[:], 1.0)
+        neg_half = held.tile([P, P], F32, name="neg_half")
+        nc.vector.memset(neg_half[:], -0.5)
         one_bf = held.tile([P, 1], BF16, name="one_bf")
-        nc.gpsimd.memset(one_bf[:], 1.0)
+        nc.vector.memset(one_bf[:], 1.0)
+        ident_bf = held.tile([P, P], BF16, name="ident_bf")
+        nc.vector.tensor_copy(ident_bf[:], ident_f[:])
+
+        ln_tf = held.tile([P, C], F32, name="ln_tf")
+        ln_df = held.tile([P, C], F32, name="ln_df")
+        nc.scalar.activation(ln_tf[:], tf_c[:], ACT.Ln, bias=1.0)
+        nc.scalar.activation(ln_df[:], df_c[:], ACT.Ln, bias=2.0)
+        inv_ln_df = held.tile([P, C], F32, name="inv_ln_df")
+        nc.vector.reciprocal(inv_ln_df[:], ln_df[:])
+        wt_c = held.tile([P, C], F32, name="wt_c")
+        nc.vector.tensor_mul(wt_c[:], ln_tf[:], inv_ln_df[:])
+
         gamma = held.tile([P, HEADS], F32, name="gamma")
-        nc.gpsimd.dma_start(gamma[:], bn_gamma.rearrange("h o -> (h o)").partition_broadcast(P))
+        nc.scalar.dma_start(gamma[:], bn_gamma.rearrange("h o -> (h o)").partition_broadcast(P))
         fcw = held.tile([P, HEADS, P], BF16, name="fcw")
-        nc.gpsimd.dma_start(fcw[:], fc_w.rearrange("(a k) m -> k a m", k=P))
+        nc.scalar.dma_start(fcw[:], fc_w.rearrange("(a k) m -> k a m", k=P))
         fcb = held.tile([P, 1], F32, name="fcb")
-        nc.gpsimd.dma_start(fcb[:], fc_b)
+        nc.scalar.dma_start(fcb[:], fc_b)
 
         keys = held.tile([P, HEADS * DOCS * T, KEYW], BF16, name="keys")
         dist = [[dists.tile([P, KEPT], F32, name=f"dist{a}{b}") for b in range(DOCS)] for a in range(HEADS)]
         sum_once = held.tile([P, HEADS * DOCS * T], F32, name="sum_once")
         sum_twice = held.tile([P, HEADS * DOCS * T], F32, name="sum_twice")
-        nc.gpsimd.memset(sum_twice[:], 0.0)
+        nc.vector.memset(sum_twice[:], 0.0)
         sqcol = held.tile([P, HEADS * DOCS * T], F32, name="sqcol")
         hsum_sq = held.tile([P, HEADS * DOCS], F32, name="hsum_sq")
 
         with (
             tc.tile_pool(name="weights", bufs=1) as weights,
-            tc.tile_pool(name="tables", bufs=2) as tables,
-            tc.tile_pool(name="work", bufs=3) as work,
-            tc.psum_pool(name="ps_gram", bufs=4) as ps_gram,
+            tc.tile_pool(name="tables", bufs=1) as tables,
+            tc.tile_pool(name="work", bufs=4) as work,
+            tc.psum_pool(name="ps_gram", bufs=5) as ps_gram,
             tc.psum_pool(name="ps_prep", bufs=1) as ps_prep,
         ):
             hsum_ps = ps_prep.tile([P, HEADS * DOCS], F32, name="hsum_ps")
+            spread = tables.tile([P, DOCS, L // C, C], F32, name="spread", offset=TABLE_BYTES)
             wt = [weights.tile([P, L], F32, name=f"wt{b}") for b in range(DOCS)]
             for b in range(DOCS):
-                nc.scalar.dma_start(
-                    wt[b][:], parked[:, b * L:(b + 1) * L].rearrange("o n -> (o n)").partition_broadcast(P)
+                nc.vector.tensor_tensor(
+                    spread[:, b],
+                    wt_c[:].unsqueeze(1).to_broadcast([P, L // C, C]),
+                    ident_f[:, b * (L // C):(b + 1) * (L // C)].unsqueeze(2).to_broadcast([P, L // C, C]),
+                    ALU.mult,
                 )
+                wt_ps = ps_gram.tile([P, L], F32, name="wt_ps", tag="gram_ps")
+                nc.tensor.matmul(wt_ps[:], ones[:], spread[:, b].rearrange("p q c -> p (q c)"), start=True, stop=True)
+                nc.scalar.activation(wt[b][:], wt_ps[:], ACT.Copy)
 
+            def prepare(a, b, table):
+                block = (a * DOCS + b) * T
+                h = work.tile([P, L], F32, name="h")
+                nc.vector.tensor_tensor(
+                    h[:],
+                    table[:].indirect(offsets[:, b * (L // 16):(b + 1) * (L // 16)]),
+                    wt[b][:],
+                    ALU.mult,
+                )
+                hb = work.tile([P, L], BF16, name="hb")
+                nc.gpsimd.tensor_copy(hb[:], h[:])
+                hsq = work.tile([P, L], F32, name="hsq")
+                nc.scalar.activation(hsq[:], h[:], ACT.Square)
+
+                sqrow_ps = ps_prep.tile([P, L], F32, name="sqrow_ps")
+                nc.tensor.matmul(sqrow_ps[:], neg_half[:], hsq[:], start=True, stop=True)
+                sqrow = work.tile([P, L], F32, name="sqrow")
+                nc.scalar.activation(sqrow[:], sqrow_ps[:], ACT.Copy)
+                for t in range(T):
+                    picked = work.tile([P, P], F32, name="picked")
+                    nc.vector.scalar_tensor_tensor(
+                        picked[:], sqrow[:, t * P:(t + 1) * P], 1.0, ident_f[:], ALU.mult, ALU.mult,
+                        accum_out=sqcol[:, block + t:block + t + 1],
+                    )
+
+                hT_ps = ps_prep.tile([P, T, P], BF16, name="hT_ps")
+                for t in range(T):
+                    nc.tensor.transpose(hT_ps[:, t, :], hb[:, t * P:(t + 1) * P], ident_bf[:])
+                nc.scalar.activation(keys[:, block:block + T, 0:P], hT_ps[:], ACT.Copy)
+                for t in range(T):
+                    nc.tensor.matmul(
+                        hsum_ps[:, a * DOCS + b:a * DOCS + b + 1], keys[:, block + t, 0:P], one_bf[:],
+                        start=(t == 0), stop=(t == T - 1),
+                    )
+                return hb, sqrow
+
+            def distances(a, b, hb, sqrow):
+                block = (a * DOCS + b) * T
+                for t in range(T):
+                    gram_ps = ps_gram.tile([P, L], F32, name="gram_ps")
+                    nc.tensor.matmul(
+                        gram_ps[:, 0:WIDTH[t]], hb[:, t * P:(t + 1) * P], hb[:, FIRST[t]:L], start=True, stop=True
+                    )
+                    nc.vector.scalar_tensor_tensor(
+                        dist[a][b][:, START[t]:START[t] + WIDTH[t]], gram_ps[:, 0:WIDTH[t]],
+                        sqcol[:, block + t:block + t + 1], sqrow[:, FIRST[t]:L], ALU.add, ALU.add,
+                    )
+                nc.vector.tensor_scalar_min(dist[a][b][:], dist[a][b][:], 0.0)
+                for t in range(T):
+                    diagonal = dist[a][b][:, START[t]:START[t] + P]
+                    nc.scalar.activation(
+                        diagonal, diagonal, ACT.Sqrt, scale=-2.0, bias=TINY,
+                        accum_out=sum_once[:, block + t:block + t + 1],
+                    )
+                    if WIDTH[t] > P:
+                        right = dist[a][b][:, START[t] + P:START[t] + WIDTH[t]]
+                        nc.scalar.activation(
+                            right, right, ACT.Sqrt, scale=-2.0, bias=TINY,
+                            accum_out=sum_twice[:, block + t:block + t + 1],
+                        )
+
+            waiting = None
             for a in range(HEADS):
-                table = tables.tile([P, S], F32, name="table")
+                table = tables.tile([P, S], F32, name=f"table{a}", offset=(a % 2) * TABLE_BYTES)
                 nc.sync.dma_start(table[:], emb[a * P:(a + 1) * P, :])
                 for b in range(DOCS):
-                    block = (a * DOCS + b) * T
-                    h = work.tile([P, L], F32, name="h")
-                    nc.vector.tensor_tensor(
-                        h[:],
-                        table[:].indirect(offsets[:, b * (L // 16):(b + 1) * (L // 16)]),
-                        wt[b][:],
-                        ALU.mult,
-                    )
-                    hb = work.tile([P, L], BF16, name="hb")
-                    nc.gpsimd.tensor_copy(hb[:], h[:])
-                    hsq = work.tile([P, L], F32, name="hsq")
-                    nc.scalar.activation(hsq[:], h[:], ACT.Square)
-
-                    sqrow_ps = ps_prep.tile([P, L], F32, name="sqrow_ps")
-                    nc.tensor.matmul(sqrow_ps[:], neg_half[:], hsq[:], start=True, stop=True)
-                    sqrow = work.tile([P, L], F32, name="sqrow")
-                    nc.scalar.activation(sqrow[:], sqrow_ps[:], ACT.Copy)
-                    sqcol_ps = ps_prep.tile([P, T], F32, name="sqcol_ps")
-                    for t in range(T):
-                        nc.tensor.matmul(
-                            sqcol_ps[:, t:t + 1], hsq[:, t * P:(t + 1) * P], neg_half[:, 0:1], start=True, stop=True
-                        )
-                    nc.scalar.activation(sqcol[:, block:block + T], sqcol_ps[:], ACT.Identity, bias=-0.5 * TINY)
-
-                    hT_ps = ps_prep.tile([P, T, P], BF16, name="hT_ps")
-                    for t in range(T):
-                        nc.tensor.transpose(hT_ps[:, t, :], hb[:, t * P:(t + 1) * P], ident_bf[:])
-                    nc.scalar.activation(keys[:, block:block + T, 0:P], hT_ps[:], ACT.Copy)
-                    for t in range(T):
-                        nc.tensor.matmul(
-                            hsum_ps[:, a * DOCS + b:a * DOCS + b + 1], keys[:, block + t, 0:P], one_bf[:],
-                            start=(t == 0), stop=(t == T - 1),
-                        )
-
-                    for t in range(T):
-                        gram_ps = ps_gram.tile([P, L], F32, name="gram_ps")
-                        nc.tensor.matmul(
-                            gram_ps[:, 0:WIDTH[t]], hb[:, t * P:(t + 1) * P], hb[:, FIRST[t]:L], start=True, stop=True
-                        )
-                        nc.vector.scalar_tensor_tensor(
-                            dist[a][b][:, START[t]:START[t] + WIDTH[t]], gram_ps[:, 0:WIDTH[t]],
-                            sqcol[:, block + t:block + t + 1], sqrow[:, FIRST[t]:L], ALU.add, ALU.add,
-                        )
-                    nc.vector.tensor_scalar_min(dist[a][b][:], dist[a][b][:], -0.5 * TINY)
-                    for t in range(T):
-                        diagonal = dist[a][b][:, START[t]:START[t] + P]
-                        nc.scalar.activation(
-                            diagonal, diagonal, ACT.Sqrt, scale=-2.0, accum_out=sum_once[:, block + t:block + t + 1]
-                        )
-                        if WIDTH[t] > P:
-                            right = dist[a][b][:, START[t] + P:START[t] + WIDTH[t]]
-                            nc.scalar.activation(
-                                right, right, ACT.Sqrt, scale=-2.0, accum_out=sum_twice[:, block + t:block + t + 1]
-                            )
+                    hb, sqrow = prepare(a, b, table)
+                    if waiting is not None:
+                        distances(*waiting)
+                    waiting = (a, b, hb, sqrow)
+            distances(*waiting)
             nc.scalar.activation(hsum_sq[:], hsum_ps[:], ACT.Square)
 
         gain = held.tile([P, HEADS], F32, name="gain")
@@ -172,7 +194,7 @@ def tile_attentiontfidf_b_kernel(tc, emb, tf, df, bn_gamma, fc_w, fc_b, offs, ou
             mean = held.tile([P, HEADS], F32, name="mean")
             nc.vector.tensor_scalar_mul(mean[:], total_ps[:, 0:HEADS], 1.0 / PAIRS)
             mean_sq = held.tile([P, HEADS], F32, name="mean_sq")
-            nc.vector.tensor_scalar_mul(mean_sq[:], total_ps[:, HEADS:2 * HEADS], -2.0 / PAIRS)
+            nc.vector.tensor_scalar(mean_sq[:], total_ps[:, HEADS:2 * HEADS], -2.0 / PAIRS, TINY, ALU.mult, ALU.add)
             sq_mean = held.tile([P, HEADS], F32, name="sq_mean")
             nc.vector.tensor_mul(sq_mean[:], mean[:], mean[:])
             var_eps = held.tile([P, HEADS], F32, name="var_eps")
@@ -186,8 +208,8 @@ def tile_attentiontfidf_b_kernel(tc, emb, tf, df, bn_gamma, fc_w, fc_b, offs, ou
 
         received = held.tile([P, HEADS * DOCS * T], F32, name="received")
         with (
-            tc.tile_pool(name="exps", bufs=3) as exps,
-            tc.tile_pool(name="small", bufs=3) as small,
+            tc.tile_pool(name="exps", bufs=4) as exps,
+            tc.tile_pool(name="small", bufs=4) as small,
             tc.tile_pool(name="vos", bufs=2 * HEADS) as vos,
             tc.tile_pool(name="outs", bufs=2) as outs,
             tc.psum_pool(name="ps_v", bufs=3) as ps_v,
@@ -195,64 +217,79 @@ def tile_attentiontfidf_b_kernel(tc, emb, tf, df, bn_gamma, fc_w, fc_b, offs, ou
             tc.psum_pool(name="ps_o", bufs=1) as ps_o,
             tc.psum_pool(name="ps_e", bufs=2) as ps_e,
         ):
-            for b in range(DOCS):
-                vo = []
-                for a in range(HEADS):
-                    block = (a * DOCS + b) * T
-                    e = exps.tile([P, T, L], BF16, name="e")
-                    right_sum = small.tile([P, T], F32, name="right_sum")
-                    for t in range(T):
-                        nc.scalar.activation(
-                            e[:, t, FIRST[t]:L], dist[a][b][:, START[t]:START[t] + WIDTH[t]], ACT.Exp,
-                            bias=shift[:, a:a + 1], scale=gain[:, a:a + 1], accum_out=right_sum[:, t:t + 1],
+            def exponentials(a, b):
+                block = (a * DOCS + b) * T
+                e = exps.tile([P, T, L], BF16, name="e")
+                right_sum = small.tile([P, T], F32, name="right_sum")
+                for t in range(T):
+                    nc.scalar.activation(
+                        e[:, t, FIRST[t]:L], dist[a][b][:, START[t]:START[t] + WIDTH[t]], ACT.Exp,
+                        bias=shift[:, a:a + 1], scale=gain[:, a:a + 1], accum_out=right_sum[:, t:t + 1],
+                    )
+                eT_ps = ps_e.tile([P, MIRRORED], BF16, name="eT_ps")
+                rowsum = small.tile([P, T], F32, name="rowsum")
+                for t in range(1, T):
+                    for s in range(t):
+                        nc.tensor.transpose(
+                            eT_ps[:, BELOW[t] + s * P:BELOW[t] + (s + 1) * P], e[:, s, t * P:(t + 1) * P], ident_bf[:]
                         )
-                    eT_ps = ps_e.tile([P, MIRRORED], BF16, name="eT_ps")
-                    rowsum = small.tile([P, T], F32, name="rowsum")
-                    for t in range(1, T):
-                        for s in range(t):
-                            nc.tensor.transpose(
-                                eT_ps[:, BELOW[t] + s * P:BELOW[t] + (s + 1) * P], e[:, s, t * P:(t + 1) * P], ident_bf[:]
+                for t in range(1, T):
+                    nc.vector.tensor_scalar(
+                        e[:, t, 0:FIRST[t]], eT_ps[:, BELOW[t]:BELOW[t] + FIRST[t]], 1.0, right_sum[:, t:t + 1],
+                        ALU.mult, ALU.add, accum_out=rowsum[:, t:t + 1],
+                    )
+                rinv = small.tile([P, T], F32, name="rinv")
+                nc.vector.reciprocal(rinv[:, 0:1], right_sum[:, 0:1])
+                nc.vector.reciprocal(rinv[:, 1:T], rowsum[:, 1:T])
+                nc.vector.tensor_copy(keys[:, block:block + T, P:P + 1].squeeze(2), rinv[:])
+                return e, rinv
+
+            def weighted_sums(a, b, e, rinv):
+                block = (a * DOCS + b) * T
+                voT = small.tile([P, T, P], BF16, name="voT")
+                for pair in range(T // 2):
+                    v_ps = ps_v.tile([P, 2, BANK // 2], F32, name="v_ps")
+                    for g in range(2):
+                        s = 2 * pair + g
+                        for t in range(T):
+                            nc.tensor.matmul(
+                                v_ps[:, g, 0:P + 1], e[:, t, s * P:(s + 1) * P], keys[:, block + t, 0:P + 1],
+                                start=(t == 0), stop=(t == T - 1),
                             )
-                    for t in range(1, T):
-                        nc.vector.tensor_scalar(
-                            e[:, t, 0:FIRST[t]], eT_ps[:, BELOW[t]:BELOW[t] + FIRST[t]], 1.0, right_sum[:, t:t + 1],
-                            ALU.mult, ALU.add, accum_out=rowsum[:, t:t + 1],
-                        )
-                    rinv = small.tile([P, T], F32, name="rinv")
-                    nc.vector.reciprocal(rinv[:, 0:1], right_sum[:, 0:1])
-                    nc.vector.reciprocal(rinv[:, 1:T], rowsum[:, 1:T])
-                    nc.vector.tensor_copy(keys[:, block:block + T, P:P + 1].squeeze(2), rinv[:])
+                    nc.vector.tensor_tensor(
+                        voT[:, 2 * pair:2 * pair + 2, :], v_ps[:, :, 0:P],
+                        rinv[:, 2 * pair:2 * pair + 2].unsqueeze(2).to_broadcast([P, 2, P]), ALU.mult,
+                    )
+                    nc.vector.tensor_copy(
+                        received[:, block + 2 * pair:block + 2 * pair + 2], v_ps[:, :, P:P + 1].squeeze(2)
+                    )
+                vo_ps = ps_t.tile([P, L], BF16, name="vo_ps")
+                for s in range(T):
+                    nc.tensor.transpose(vo_ps[:, s * P:(s + 1) * P], voT[:, s, :], ident_bf[:])
+                vo_a = vos.tile([P, L], BF16, name="vo_a")
+                nc.scalar.activation(vo_a[:], vo_ps[:], ACT.Copy)
+                return vo_a
 
-                    voT = small.tile([P, T, P], BF16, name="voT")
-                    for pair in range(T // 2):
-                        v_ps = ps_v.tile([P, 2, BANK // 2], F32, name="v_ps")
-                        for g in range(2):
-                            s = 2 * pair + g
-                            for t in range(T):
-                                nc.tensor.matmul(
-                                    v_ps[:, g, 0:P + 1], e[:, t, s * P:(s + 1) * P], keys[:, block + t, 0:P + 1],
-                                    start=(t == 0), stop=(t == T - 1),
-                                )
-                        nc.vector.tensor_tensor(
-                            voT[:, 2 * pair:2 * pair + 2, :], v_ps[:, :, 0:P],
-                            rinv[:, 2 * pair:2 * pair + 2].unsqueeze(2).to_broadcast([P, 2, P]), ALU.mult,
-                        )
-                        nc.vector.tensor_copy(
-                            received[:, block + 2 * pair:block + 2 * pair + 2], v_ps[:, :, P:P + 1].squeeze(2)
-                        )
-                    vo_ps = ps_t.tile([P, L], BF16, name="vo_ps")
-                    for s in range(T):
-                        nc.tensor.transpose(vo_ps[:, s * P:(s + 1) * P], voT[:, s, :], ident_bf[:])
-                    vo_a = vos.tile([P, L], BF16, name="vo_a")
-                    nc.scalar.activation(vo_a[:], vo_ps[:], ACT.Copy)
-                    vo.append(vo_a)
-
+            def class_scores(b, vo):
                 lg_ps = ps_o.tile([P, L], F32, name="lg_ps")
                 for a in range(HEADS):
                     nc.tensor.matmul(lg_ps[:], fcw[:, a, :], vo[a][:], start=(a == 0), stop=(a == HEADS - 1))
                 lg = outs.tile([P, L], F32, name="lg")
                 nc.vector.tensor_scalar_add(lg[:], lg_ps[:], fcb[:, 0:1])
                 nc.sync.dma_start(out[0:P, b * L:(b + 1) * L], lg[:])
+
+            vo = [[] for b in range(DOCS)]
+            waiting = None
+            for b in range(DOCS):
+                for a in range(HEADS):
+                    e, rinv = exponentials(a, b)
+                    if waiting is not None:
+                        vo[waiting[1]].append(weighted_sums(*waiting))
+                        if len(vo[waiting[1]]) == HEADS:
+                            class_scores(waiting[1], vo[waiting[1]])
+                    waiting = (a, b, e, rinv)
+            vo[DOCS - 1].append(weighted_sums(*waiting))
+            class_scores(DOCS - 1, vo[DOCS - 1])
 
             received_sum = small.tile([P, DOCS * T], F32, name="received_sum")
             nc.vector.tensor_reduce(

@@ -110,7 +110,7 @@ def tile_attentiontfidf_b_kernel(tc, emb, tf, df, bn_gamma, fc_w, fc_b, offs, ou
                     ALU.mult,
                 )
                 hb = work.tile([P, L], BF16, name="hb")
-                nc.gpsimd.tensor_copy(hb[:], h[:])
+                nc.vector.tensor_copy(hb[:], h[:])
                 hsq = work.tile([P, L], F32, name="hsq")
                 nc.scalar.activation(hsq[:], h[:], ACT.Square)
 

@@ -19,6 +19,7 @@ PAIRS = DOCS * L * L
 EPS_BN, TINY = 1e-5, 1e-12
 KEYW = 144
 BANK = 512
+PARTS = 3
 
 FIRST = [t * P for t in range(T)]
 WIDTH = [L - first for first in FIRST]
@@ -48,7 +49,7 @@ def tile_attentiontfidf_b_kernel(tc, emb, tf, df, bn_gamma, fc_w, fc_b, offs, ou
         make_identity(nc, ident_f[:])
         ones = held.tile([P, P], F32, name="ones")
         nc.vector.memset(ones[:], 1.0)
-        neg_half = held.tile([P, P], F32, name="neg_half")
+        neg_half = held.tile([P, 1], F32, name="neg_half")
         nc.vector.memset(neg_half[:], -0.5)
         one_bf = held.tile([P, 1], BF16, name="one_bf")
         nc.vector.memset(one_bf[:], 1.0)
@@ -79,14 +80,28 @@ def tile_attentiontfidf_b_kernel(tc, emb, tf, df, bn_gamma, fc_w, fc_b, offs, ou
         sqcol = held.tile([P, HEADS * DOCS * T], F32, name="sqcol")
         hsum_sq = held.tile([P, HEADS * DOCS], F32, name="hsum_sq")
 
+        parts = [held.tile([P, T, P], BF16, name=f"parts{a}") for a in range(HEADS)]
+        for a in range(HEADS):
+            nc.gpsimd.memset(parts[a][:], 0.0)
+        chosen_rows = held.tile([P, DOCS], F32, name="chosen_rows")
+        nc.vector.tensor_reduce(
+            chosen_rows[:], ident_f[:, 0:PARTS * DOCS].rearrange("p (r b) -> p b r", b=DOCS), AX.X, ALU.add
+        )
+        choose = [held.tile([P, P], BF16, name=f"choose{b}") for b in range(DOCS)]
+        for b in range(DOCS):
+            nc.vector.tensor_scalar_mul(choose[b][:], ones[:], chosen_rows[:, b:b + 1])
+
         with (
             tc.tile_pool(name="weights", bufs=1) as weights,
             tc.tile_pool(name="tables", bufs=1) as tables,
             tc.tile_pool(name="work", bufs=4) as work,
+            tc.tile_pool(name="heads", bufs=HEADS) as heads,
+            tc.tile_pool(name="rounded", bufs=HEADS * DOCS) as rounded,
             tc.psum_pool(name="ps_gram", bufs=5) as ps_gram,
             tc.psum_pool(name="ps_prep", bufs=1) as ps_prep,
         ):
-            hsum_ps = ps_prep.tile([P, HEADS * DOCS], F32, name="hsum_ps")
+            column_ps = ps_prep.tile([P, 2 * HEADS * DOCS * T], F32, name="column_ps")
+            hsum_ps = column_ps[:, HEADS * DOCS * T:2 * HEADS * DOCS * T]
             spread = tables.tile([P, DOCS, L // C, C], F32, name="spread", offset=TABLE_BYTES)
             wt = [weights.tile([P, L], F32, name=f"wt{b}") for b in range(DOCS)]
             for b in range(DOCS):
@@ -100,7 +115,7 @@ def tile_attentiontfidf_b_kernel(tc, emb, tf, df, bn_gamma, fc_w, fc_b, offs, ou
                 nc.tensor.matmul(wt_ps[:], ones[:], spread[:, b].rearrange("p q c -> p (q c)"), start=True, stop=True)
                 nc.scalar.activation(wt[b][:], wt_ps[:], ACT.Copy)
 
-            def prepare(a, b, table):
+            def look_up(a, b, table):
                 block = (a * DOCS + b) * T
                 h = work.tile([P, L], F32, name="h")
                 nc.vector.tensor_tensor(
@@ -109,20 +124,14 @@ def tile_attentiontfidf_b_kernel(tc, emb, tf, df, bn_gamma, fc_w, fc_b, offs, ou
                     wt[b][:],
                     ALU.mult,
                 )
-                hb = work.tile([P, L], BF16, name="hb")
+                hb = rounded.tile([P, L], BF16, name="hb")
                 nc.vector.tensor_copy(hb[:], h[:])
                 hsq = work.tile([P, L], F32, name="hsq")
                 nc.scalar.activation(hsq[:], h[:], ACT.Square)
-
-                sqrow_ps = ps_prep.tile([P, L], F32, name="sqrow_ps")
-                nc.tensor.matmul(sqrow_ps[:], neg_half[:], hsq[:], start=True, stop=True)
-                sqrow = work.tile([P, L], F32, name="sqrow")
-                nc.scalar.activation(sqrow[:], sqrow_ps[:], ACT.Copy)
                 for t in range(T):
-                    picked = work.tile([P, P], F32, name="picked")
-                    nc.vector.scalar_tensor_tensor(
-                        picked[:], sqrow[:, t * P:(t + 1) * P], 1.0, ident_f[:], ALU.mult, ALU.mult,
-                        accum_out=sqcol[:, block + t:block + t + 1],
+                    nc.tensor.matmul(
+                        column_ps[:, block + t:block + t + 1], hsq[:, t * P:(t + 1) * P], neg_half[:],
+                        start=True, stop=True,
                     )
 
                 hT_ps = ps_prep.tile([P, T, P], BF16, name="hT_ps")
@@ -131,23 +140,45 @@ def tile_attentiontfidf_b_kernel(tc, emb, tf, df, bn_gamma, fc_w, fc_b, offs, ou
                 nc.scalar.activation(keys[:, block:block + T, 0:P], hT_ps[:], ACT.Copy)
                 for t in range(T):
                     nc.tensor.matmul(
-                        hsum_ps[:, a * DOCS + b:a * DOCS + b + 1], keys[:, block + t, 0:P], one_bf[:],
-                        start=(t == 0), stop=(t == T - 1),
+                        hsum_ps[:, block + t:block + t + 1], keys[:, block + t, 0:P], one_bf[:], start=True, stop=True
                     )
-                return hb, sqrow
+                return hb
 
-            def distances(a, b, hb, sqrow):
+            def rows_of_squares(a):
+                first = a * DOCS * T
+                mine = sqcol[:, first:first + DOCS * T]
+                nc.vector.tensor_copy(mine, column_ps[:, first:first + DOCS * T])
+
+                def part(r):
+                    return parts[a][:, :, r * DOCS:(r + 1) * DOCS]
+
+                def by_block(columns):
+                    return columns.rearrange("p (b t) -> p t b", t=T)
+
+                rest1 = heads.tile([P, DOCS * T], F32, name="rest1")
+                nc.vector.tensor_copy(part(0), by_block(mine))
+                nc.vector.tensor_tensor(by_block(rest1[:]), by_block(mine), part(0), ALU.subtract)
+                nc.vector.tensor_copy(part(1), by_block(rest1[:]))
+                nc.vector.tensor_tensor(part(2), by_block(rest1[:]), part(1), ALU.subtract)
+                rows_ps = ps_prep.tile([P, L], F32, name="rows_ps")
+                for t in range(T):
+                    nc.tensor.matmul(rows_ps[:, t * P:(t + 1) * P], parts[a][:, t, :], ident_bf[:], start=True, stop=True)
+                rows = heads.tile([P, L], BF16, name="rows")
+                nc.scalar.activation(rows[:], rows_ps[:], ACT.Copy)
+                return rows
+
+            def distances(a, b, hb, rows):
                 block = (a * DOCS + b) * T
                 for t in range(T):
                     gram_ps = ps_gram.tile([P, L], F32, name="gram_ps")
+                    nc.tensor.matmul(gram_ps[:, 0:WIDTH[t]], choose[b][:], rows[:, FIRST[t]:L], start=True, stop=False)
                     nc.tensor.matmul(
-                        gram_ps[:, 0:WIDTH[t]], hb[:, t * P:(t + 1) * P], hb[:, FIRST[t]:L], start=True, stop=True
+                        gram_ps[:, 0:WIDTH[t]], hb[:, t * P:(t + 1) * P], hb[:, FIRST[t]:L], start=False, stop=True
                     )
-                    nc.vector.scalar_tensor_tensor(
+                    nc.vector.tensor_scalar(
                         dist[a][b][:, START[t]:START[t] + WIDTH[t]], gram_ps[:, 0:WIDTH[t]],
-                        sqcol[:, block + t:block + t + 1], sqrow[:, FIRST[t]:L], ALU.add, ALU.add,
+                        sqcol[:, block + t:block + t + 1], 0.0, ALU.add, ALU.min,
                     )
-                nc.vector.tensor_scalar_min(dist[a][b][:], dist[a][b][:], 0.0)
                 for t in range(T):
                     diagonal = dist[a][b][:, START[t]:START[t] + P]
                     nc.scalar.activation(
@@ -161,17 +192,19 @@ def tile_attentiontfidf_b_kernel(tc, emb, tf, df, bn_gamma, fc_w, fc_b, offs, ou
                             accum_out=sum_twice[:, block + t:block + t + 1],
                         )
 
-            waiting = None
+            hb, rows = {}, {}
             for a in range(HEADS):
                 table = tables.tile([P, S], F32, name=f"table{a}", offset=(a % 2) * TABLE_BYTES)
                 nc.sync.dma_start(table[:], emb[a * P:(a + 1) * P, :])
                 for b in range(DOCS):
-                    hb, sqrow = prepare(a, b, table)
-                    if waiting is not None:
-                        distances(*waiting)
-                    waiting = (a, b, hb, sqrow)
-            distances(*waiting)
-            nc.scalar.activation(hsum_sq[:], hsum_ps[:], ACT.Square)
+                    hb[a, b] = look_up(a, b, table)
+                rows[a] = rows_of_squares(a)
+            for a in range(HEADS):
+                for b in range(DOCS):
+                    distances(a, b, hb[a, b], rows[a])
+            hsum = held.tile([P, HEADS * DOCS], F32, name="hsum")
+            nc.vector.tensor_reduce(hsum[:], hsum_ps.rearrange("p (c t) -> p c t", t=T), AX.X, ALU.add)
+            nc.vector.tensor_mul(hsum_sq[:], hsum[:], hsum[:])
 
         gain = held.tile([P, HEADS], F32, name="gain")
         shift = held.tile([P, HEADS], F32, name="shift")

@@ -49,8 +49,6 @@ def tile_attentiontfidf_b_kernel(tc, emb, tf, df, bn_gamma, fc_w, fc_b, offs, ou
         make_identity(nc, ident_f[:])
         ones = held.tile([P, P], F32, name="ones")
         nc.vector.memset(ones[:], 1.0)
-        neg_half = held.tile([P, 1], F32, name="neg_half")
-        nc.vector.memset(neg_half[:], -0.5)
         one_bf = held.tile([P, 1], BF16, name="one_bf")
         nc.vector.memset(one_bf[:], 1.0)
         ident_bf = held.tile([P, P], BF16, name="ident_bf")
@@ -77,6 +75,7 @@ def tile_attentiontfidf_b_kernel(tc, emb, tf, df, bn_gamma, fc_w, fc_b, offs, ou
         sum_once = held.tile([P, HEADS * DOCS * T], F32, name="sum_once")
         sum_twice = held.tile([P, HEADS * DOCS * T], F32, name="sum_twice")
         nc.vector.memset(sum_twice[:], 0.0)
+        sq = held.tile([P, HEADS * DOCS * T], F32, name="sq")
         sqcol = held.tile([P, HEADS * DOCS * T], F32, name="sqcol")
         hsum_sq = held.tile([P, HEADS * DOCS], F32, name="hsum_sq")
 
@@ -98,10 +97,10 @@ def tile_attentiontfidf_b_kernel(tc, emb, tf, df, bn_gamma, fc_w, fc_b, offs, ou
             tc.tile_pool(name="heads", bufs=HEADS) as heads,
             tc.tile_pool(name="rounded", bufs=HEADS * DOCS) as rounded,
             tc.psum_pool(name="ps_gram", bufs=5) as ps_gram,
+            tc.psum_pool(name="ps_turn", bufs=2) as ps_turn,
             tc.psum_pool(name="ps_prep", bufs=1) as ps_prep,
         ):
-            column_ps = ps_prep.tile([P, 2 * HEADS * DOCS * T], F32, name="column_ps")
-            hsum_ps = column_ps[:, HEADS * DOCS * T:2 * HEADS * DOCS * T]
+            hsum_ps = ps_prep.tile([P, HEADS * DOCS * T], F32, name="hsum_ps")
             spread = tables.tile([P, DOCS, L // C, C], F32, name="spread", offset=TABLE_BYTES)
             wt = [weights.tile([P, L], F32, name=f"wt{b}") for b in range(DOCS)]
             for b in range(DOCS):
@@ -126,17 +125,14 @@ def tile_attentiontfidf_b_kernel(tc, emb, tf, df, bn_gamma, fc_w, fc_b, offs, ou
                 )
                 hb = rounded.tile([P, L], BF16, name="hb")
                 nc.vector.tensor_copy(hb[:], h[:])
-                hsq = work.tile([P, L], F32, name="hsq")
-                nc.scalar.activation(hsq[:], h[:], ACT.Square)
+                hT_ps = ps_turn.tile([P, T, P], F32, name="hT_ps")
                 for t in range(T):
-                    nc.tensor.matmul(
-                        column_ps[:, block + t:block + t + 1], hsq[:, t * P:(t + 1) * P], neg_half[:],
-                        start=True, stop=True,
+                    nc.tensor.transpose(hT_ps[:, t, :], h[:, t * P:(t + 1) * P], ident_f[:])
+                for t in range(T):
+                    squares = work.tile([P, P], F32, name="squares")
+                    nc.scalar.activation(
+                        squares[:], hT_ps[:, t, :], ACT.Square, accum_out=sq[:, block + t:block + t + 1]
                     )
-
-                hT_ps = ps_prep.tile([P, T, P], BF16, name="hT_ps")
-                for t in range(T):
-                    nc.tensor.transpose(hT_ps[:, t, :], hb[:, t * P:(t + 1) * P], ident_bf[:])
                 nc.scalar.activation(keys[:, block:block + T, 0:P], hT_ps[:], ACT.Copy)
                 for t in range(T):
                     nc.tensor.matmul(
@@ -147,7 +143,7 @@ def tile_attentiontfidf_b_kernel(tc, emb, tf, df, bn_gamma, fc_w, fc_b, offs, ou
             def rows_of_squares(a):
                 first = a * DOCS * T
                 mine = sqcol[:, first:first + DOCS * T]
-                nc.vector.tensor_copy(mine, column_ps[:, first:first + DOCS * T])
+                nc.vector.tensor_scalar_mul(mine, sq[:, first:first + DOCS * T], -0.5)
 
                 def part(r):
                     return parts[a][:, :, r * DOCS:(r + 1) * DOCS]
@@ -160,7 +156,7 @@ def tile_attentiontfidf_b_kernel(tc, emb, tf, df, bn_gamma, fc_w, fc_b, offs, ou
                 nc.vector.tensor_tensor(by_block(rest1[:]), by_block(mine), part(0), ALU.subtract)
                 nc.vector.tensor_copy(part(1), by_block(rest1[:]))
                 nc.vector.tensor_tensor(part(2), by_block(rest1[:]), part(1), ALU.subtract)
-                rows_ps = ps_prep.tile([P, L], F32, name="rows_ps")
+                rows_ps = ps_gram.tile([P, L], F32, name="rows_ps", tag="gram_ps")
                 for t in range(T):
                     nc.tensor.matmul(rows_ps[:, t * P:(t + 1) * P], parts[a][:, t, :], ident_bf[:], start=True, stop=True)
                 rows = heads.tile([P, L], BF16, name="rows")
@@ -203,7 +199,7 @@ def tile_attentiontfidf_b_kernel(tc, emb, tf, df, bn_gamma, fc_w, fc_b, offs, ou
                 for b in range(DOCS):
                     distances(a, b, hb[a, b], rows[a])
             hsum = held.tile([P, HEADS * DOCS], F32, name="hsum")
-            nc.vector.tensor_reduce(hsum[:], hsum_ps.rearrange("p (c t) -> p c t", t=T), AX.X, ALU.add)
+            nc.vector.tensor_reduce(hsum[:], hsum_ps[:].rearrange("p (c t) -> p c t", t=T), AX.X, ALU.add)
             nc.vector.tensor_mul(hsum_sq[:], hsum[:], hsum[:])
 
         gain = held.tile([P, HEADS], F32, name="gain")
@@ -251,7 +247,6 @@ def tile_attentiontfidf_b_kernel(tc, emb, tf, df, bn_gamma, fc_w, fc_b, offs, ou
             tc.psum_pool(name="ps_e", bufs=2) as ps_e,
         ):
             def exponentials(a, b):
-                block = (a * DOCS + b) * T
                 e = exps.tile([P, T, L], BF16, name="e")
                 right_sum = small.tile([P, T], F32, name="right_sum")
                 for t in range(T):
@@ -259,6 +254,10 @@ def tile_attentiontfidf_b_kernel(tc, emb, tf, df, bn_gamma, fc_w, fc_b, offs, ou
                         e[:, t, FIRST[t]:L], dist[a][b][:, START[t]:START[t] + WIDTH[t]], ACT.Exp,
                         bias=shift[:, a:a + 1], scale=gain[:, a:a + 1], accum_out=right_sum[:, t:t + 1],
                     )
+                return e, right_sum
+
+            def mirror(a, b, e, right_sum):
+                block = (a * DOCS + b) * T
                 eT_ps = ps_e.tile([P, MIRRORED], BF16, name="eT_ps")
                 rowsum = small.tile([P, T], F32, name="rowsum")
                 for t in range(1, T):
@@ -275,7 +274,7 @@ def tile_attentiontfidf_b_kernel(tc, emb, tf, df, bn_gamma, fc_w, fc_b, offs, ou
                 nc.vector.reciprocal(rinv[:, 0:1], right_sum[:, 0:1])
                 nc.vector.reciprocal(rinv[:, 1:T], rowsum[:, 1:T])
                 nc.vector.tensor_copy(keys[:, block:block + T, P:P + 1].squeeze(2), rinv[:])
-                return e, rinv
+                return rinv
 
             def weighted_sums(a, b, e, rinv):
                 block = (a * DOCS + b) * T
@@ -296,11 +295,14 @@ def tile_attentiontfidf_b_kernel(tc, emb, tf, df, bn_gamma, fc_w, fc_b, offs, ou
                     nc.vector.tensor_copy(
                         received[:, block + 2 * pair:block + 2 * pair + 2], v_ps[:, :, P:P + 1].squeeze(2)
                     )
+                return voT
+
+            def channels_first(voT):
                 vo_ps = ps_t.tile([P, L], BF16, name="vo_ps")
                 for s in range(T):
                     nc.tensor.transpose(vo_ps[:, s * P:(s + 1) * P], voT[:, s, :], ident_bf[:])
                 vo_a = vos.tile([P, L], BF16, name="vo_a")
-                nc.scalar.activation(vo_a[:], vo_ps[:], ACT.Copy)
+                nc.vector.tensor_copy(vo_a[:], vo_ps[:])
                 return vo_a
 
             def class_scores(b, vo):
@@ -311,18 +313,24 @@ def tile_attentiontfidf_b_kernel(tc, emb, tf, df, bn_gamma, fc_w, fc_b, offs, ou
                 nc.vector.tensor_scalar_add(lg[:], lg_ps[:], fcb[:, 0:1])
                 nc.sync.dma_start(out[0:P, b * L:(b + 1) * L], lg[:])
 
+            units = [(a, b) for b in range(DOCS) for a in range(HEADS)]
+            e_of, right_sum_of, rinv_of, voT_of = {}, {}, {}, {}
             vo = [[] for b in range(DOCS)]
-            waiting = None
-            for b in range(DOCS):
-                for a in range(HEADS):
-                    e, rinv = exponentials(a, b)
-                    if waiting is not None:
-                        vo[waiting[1]].append(weighted_sums(*waiting))
-                        if len(vo[waiting[1]]) == HEADS:
-                            class_scores(waiting[1], vo[waiting[1]])
-                    waiting = (a, b, e, rinv)
-            vo[DOCS - 1].append(weighted_sums(*waiting))
-            class_scores(DOCS - 1, vo[DOCS - 1])
+            for step in range(len(units) + 3):
+                if step < len(units):
+                    a, b = units[step]
+                    e_of[step], right_sum_of[step] = exponentials(a, b)
+                if 0 <= step - 1 < len(units):
+                    a, b = units[step - 1]
+                    rinv_of[step - 1] = mirror(a, b, e_of[step - 1], right_sum_of[step - 1])
+                if 0 <= step - 2 < len(units):
+                    a, b = units[step - 2]
+                    voT_of[step - 2] = weighted_sums(a, b, e_of[step - 2], rinv_of[step - 2])
+                if 0 <= step - 3 < len(units):
+                    a, b = units[step - 3]
+                    vo[b].append(channels_first(voT_of[step - 3]))
+                    if len(vo[b]) == HEADS:
+                        class_scores(b, vo[b])
 
             received_sum = small.tile([P, DOCS * T], F32, name="received_sum")
             nc.vector.tensor_reduce(

@@ -23,10 +23,27 @@ PARTS = 3
 
 FIRST = [t * P for t in range(T)]
 WIDTH = [L - first for first in FIRST]
-START = [sum(WIDTH[:t]) for t in range(T)]
 KEPT = sum(WIDTH)
+ROW_ORDER = [3, 0, 1, 2]
+DIAGONAL_LAST = [t == 1 for t in range(T)]
+START = [sum(WIDTH[r] for r in ROW_ORDER[:ROW_ORDER.index(t)]) for t in range(T)]
+RUNS = [(0, 2 * P, True), (2 * P, 5 * P, False), (7 * P, 2 * P, True), (9 * P, P, False)]
 BELOW = [sum(FIRST[:t]) for t in range(T)]
 MIRRORED = sum(FIRST)
+
+
+def pieces(t):
+    if DIAGONAL_LAST[t]:
+        return [(0, t + 1, T - t - 1), ((T - t - 1) * P, t, 1)]
+    return [(0, t, T - t)]
+
+
+def kept_at(t, s):
+    for offset, first, count in pieces(t):
+        if first <= s < first + count:
+            return offset + (s - first) * P
+    raise ValueError("not kept")
+
 
 FLOPS = 2 * (2 * HEADS * DOCS * L * L * P) + 2 * (HEADS * P) * P * N
 BYTES = 4 * HEADS * P * N + 2 * 4 * N + 2 * N + 2 * HEADS * P * P + 4 * (P + 1) * N
@@ -72,9 +89,8 @@ def tile_attentiontfidf_b_kernel(tc, emb, tf, df, bn_gamma, fc_w, fc_b, offs, ou
 
         keys = held.tile([P, HEADS * DOCS * T, KEYW], BF16, name="keys")
         dist = [[dists.tile([P, KEPT], F32, name=f"dist{a}{b}") for b in range(DOCS)] for a in range(HEADS)]
-        sum_once = held.tile([P, HEADS * DOCS * T], F32, name="sum_once")
-        sum_twice = held.tile([P, HEADS * DOCS * T], F32, name="sum_twice")
-        nc.vector.memset(sum_twice[:], 0.0)
+        sum_once = held.tile([P, HEADS * DOCS * 2], F32, name="sum_once")
+        sum_twice = held.tile([P, HEADS * DOCS * 2], F32, name="sum_twice")
         sq = held.tile([P, HEADS * DOCS * T], F32, name="sq")
         sqcol = held.tile([P, HEADS * DOCS * T], F32, name="sqcol")
         hsum_sq = held.tile([P, HEADS * DOCS], F32, name="hsum_sq")
@@ -165,28 +181,27 @@ def tile_attentiontfidf_b_kernel(tc, emb, tf, df, bn_gamma, fc_w, fc_b, offs, ou
 
             def distances(a, b, hb, rows):
                 block = (a * DOCS + b) * T
-                for t in range(T):
+                for t in ROW_ORDER:
                     gram_ps = ps_gram.tile([P, L], F32, name="gram_ps")
-                    nc.tensor.matmul(gram_ps[:, 0:WIDTH[t]], choose[b][:], rows[:, FIRST[t]:L], start=True, stop=False)
-                    nc.tensor.matmul(
-                        gram_ps[:, 0:WIDTH[t]], hb[:, t * P:(t + 1) * P], hb[:, FIRST[t]:L], start=False, stop=True
-                    )
+                    for offset, first, count in pieces(t):
+                        group = gram_ps[:, offset:offset + count * P]
+                        nc.tensor.matmul(group, choose[b][:], rows[:, first * P:(first + count) * P], start=True, stop=False)
+                        nc.tensor.matmul(
+                            group, hb[:, t * P:(t + 1) * P], hb[:, first * P:(first + count) * P], start=False, stop=True
+                        )
                     nc.vector.tensor_scalar(
                         dist[a][b][:, START[t]:START[t] + WIDTH[t]], gram_ps[:, 0:WIDTH[t]],
                         sqcol[:, block + t:block + t + 1], 0.0, ALU.add, ALU.min,
                     )
-                for t in range(T):
-                    diagonal = dist[a][b][:, START[t]:START[t] + P]
+                seen = {True: 0, False: 0}
+                for begin, width, diagonal in RUNS:
+                    column = (a * DOCS + b) * 2 + seen[diagonal]
+                    seen[diagonal] += 1
+                    run = dist[a][b][:, begin:begin + width]
                     nc.scalar.activation(
-                        diagonal, diagonal, ACT.Sqrt, scale=-2.0, bias=TINY,
-                        accum_out=sum_once[:, block + t:block + t + 1],
+                        run, run, ACT.Sqrt, scale=-2.0, bias=TINY,
+                        accum_out=(sum_once if diagonal else sum_twice)[:, column:column + 1],
                     )
-                    if WIDTH[t] > P:
-                        right = dist[a][b][:, START[t] + P:START[t] + WIDTH[t]]
-                        nc.scalar.activation(
-                            right, right, ACT.Sqrt, scale=-2.0, bias=TINY,
-                            accum_out=sum_twice[:, block + t:block + t + 1],
-                        )
 
             hb, rows = {}, {}
             for a in range(HEADS):
@@ -246,6 +261,10 @@ def tile_attentiontfidf_b_kernel(tc, emb, tf, df, bn_gamma, fc_w, fc_b, offs, ou
             tc.psum_pool(name="ps_o", bufs=1) as ps_o,
             tc.psum_pool(name="ps_e", bufs=2) as ps_e,
         ):
+            def block_of(e, t, s):
+                begin = s * P if s < t else FIRST[t] + kept_at(t, s)
+                return e[:, t, begin:begin + P]
+
             def exponentials(a, b):
                 e = exps.tile([P, T, L], BF16, name="e")
                 right_sum = small.tile([P, T], F32, name="right_sum")
@@ -263,7 +282,7 @@ def tile_attentiontfidf_b_kernel(tc, emb, tf, df, bn_gamma, fc_w, fc_b, offs, ou
                 for t in range(1, T):
                     for s in range(t):
                         nc.tensor.transpose(
-                            eT_ps[:, BELOW[t] + s * P:BELOW[t] + (s + 1) * P], e[:, s, t * P:(t + 1) * P], ident_bf[:]
+                            eT_ps[:, BELOW[t] + s * P:BELOW[t] + (s + 1) * P], block_of(e, s, t), ident_bf[:]
                         )
                 for t in range(1, T):
                     nc.vector.tensor_scalar(
@@ -285,7 +304,7 @@ def tile_attentiontfidf_b_kernel(tc, emb, tf, df, bn_gamma, fc_w, fc_b, offs, ou
                         s = 2 * pair + g
                         for t in range(T):
                             nc.tensor.matmul(
-                                v_ps[:, g, 0:P + 1], e[:, t, s * P:(s + 1) * P], keys[:, block + t, 0:P + 1],
+                                v_ps[:, g, 0:P + 1], block_of(e, t, s), keys[:, block + t, 0:P + 1],
                                 start=(t == 0), stop=(t == T - 1),
                             )
                     nc.vector.tensor_tensor(

@@ -268,17 +268,18 @@ def tile_attentiontfidf_b_kernel(tc, emb, tf, df, bn_gamma, fc_w, fc_b, offs, ou
             def exponentials(a, b):
                 e = exps.tile([P, T, L], BF16, name="e")
                 right_sum = small.tile([P, T], F32, name="right_sum")
+                rowsum = small.tile([P, T], F32, name="rowsum")
                 for t in range(T):
                     nc.scalar.activation(
                         e[:, t, FIRST[t]:L], dist[a][b][:, START[t]:START[t] + WIDTH[t]], ACT.Exp,
-                        bias=shift[:, a:a + 1], scale=gain[:, a:a + 1], accum_out=right_sum[:, t:t + 1],
+                        bias=shift[:, a:a + 1], scale=gain[:, a:a + 1],
+                        accum_out=(rowsum if t == 0 else right_sum)[:, t:t + 1],
                     )
-                return e, right_sum
+                return e, right_sum, rowsum
 
-            def mirror(a, b, e, right_sum):
+            def mirror(a, b, e, right_sum, rowsum):
                 block = (a * DOCS + b) * T
                 eT_ps = ps_e.tile([P, MIRRORED], BF16, name="eT_ps")
-                rowsum = small.tile([P, T], F32, name="rowsum")
                 for t in range(1, T):
                     for s in range(t):
                         nc.tensor.transpose(
@@ -290,8 +291,7 @@ def tile_attentiontfidf_b_kernel(tc, emb, tf, df, bn_gamma, fc_w, fc_b, offs, ou
                         ALU.mult, ALU.add, accum_out=rowsum[:, t:t + 1],
                     )
                 rinv = small.tile([P, T], F32, name="rinv")
-                nc.vector.reciprocal(rinv[:, 0:1], right_sum[:, 0:1])
-                nc.vector.reciprocal(rinv[:, 1:T], rowsum[:, 1:T])
+                nc.vector.reciprocal(rinv[:], rowsum[:])
                 nc.vector.tensor_copy(keys[:, block:block + T, P:P + 1].squeeze(2), rinv[:])
                 return rinv
 
@@ -333,15 +333,15 @@ def tile_attentiontfidf_b_kernel(tc, emb, tf, df, bn_gamma, fc_w, fc_b, offs, ou
                 nc.sync.dma_start(out[0:P, b * L:(b + 1) * L], lg[:])
 
             units = [(a, b) for b in range(DOCS) for a in range(HEADS)]
-            e_of, right_sum_of, rinv_of, voT_of = {}, {}, {}, {}
+            e_of, sums_of, rinv_of, voT_of = {}, {}, {}, {}
             vo = [[] for b in range(DOCS)]
             for step in range(len(units) + 3):
                 if step < len(units):
                     a, b = units[step]
-                    e_of[step], right_sum_of[step] = exponentials(a, b)
+                    e_of[step], *sums_of[step] = exponentials(a, b)
                 if 0 <= step - 1 < len(units):
                     a, b = units[step - 1]
-                    rinv_of[step - 1] = mirror(a, b, e_of[step - 1], right_sum_of[step - 1])
+                    rinv_of[step - 1] = mirror(a, b, e_of[step - 1], *sums_of[step - 1])
                 if 0 <= step - 2 < len(units):
                     a, b = units[step - 2]
                     voT_of[step - 2] = weighted_sums(a, b, e_of[step - 2], rinv_of[step - 2])

@@ -14,10 +14,12 @@ T = L // P
 S = 4096
 N = DOCS * L
 C = N // P
+DF_AT = 32
 TABLE_BYTES = 4 * S
 PAIRS = DOCS * L * L
 EPS_BN, TINY = 1e-5, 1e-12
 KEYW = 144
+LEAD = 2 * DOCS
 BANK = 512
 PARTS = 3
 
@@ -55,13 +57,6 @@ def tile_attentiontfidf_b_kernel(tc, emb, tf, df, bn_gamma, fc_w, fc_b, offs, ou
         tc.tile_pool(name="held", bufs=1) as held,
         tc.tile_pool(name="dists", bufs=1) as dists,
     ):
-        tf_c = held.tile([P, C], F32, name="tf_c")
-        df_c = held.tile([P, C], F32, name="df_c")
-        nc.sync.dma_start(tf_c[:], tf.rearrange("o (p c) -> (o p) c", p=P))
-        nc.scalar.dma_start(df_c[:], df.rearrange("o (p c) -> (o p) c", p=P))
-        offsets = held.tile([P, N // 16], U16, name="offsets")
-        nc.sync.dma_start(offsets[:], offs)
-
         ident_f = held.tile([P, P], F32, name="ident_f")
         make_identity(nc, ident_f[:])
         ones = held.tile([P, P], F32, name="ones")
@@ -71,14 +66,12 @@ def tile_attentiontfidf_b_kernel(tc, emb, tf, df, bn_gamma, fc_w, fc_b, offs, ou
         ident_bf = held.tile([P, P], BF16, name="ident_bf")
         nc.vector.tensor_copy(ident_bf[:], ident_f[:])
 
-        ln_tf = held.tile([P, C], F32, name="ln_tf")
-        ln_df = held.tile([P, C], F32, name="ln_df")
-        nc.scalar.activation(ln_tf[:], tf_c[:], ACT.Ln, bias=1.0)
-        nc.scalar.activation(ln_df[:], df_c[:], ACT.Ln, bias=2.0)
-        inv_ln_df = held.tile([P, C], F32, name="inv_ln_df")
-        nc.vector.reciprocal(inv_ln_df[:], ln_df[:])
-        wt_c = held.tile([P, C], F32, name="wt_c")
-        nc.vector.tensor_mul(wt_c[:], ln_tf[:], inv_ln_df[:])
+        counts = held.tile([P, P], F32, name="counts")
+        nc.vector.memset(counts[:], 0.0)
+        nc.sync.dma_start(counts[0:C, :], tf.rearrange("o (c p) -> (o c) p", p=P))
+        nc.scalar.dma_start(counts[DF_AT:DF_AT + C, :], df.rearrange("o (c p) -> (o c) p", p=P))
+        offsets = held.tile([P, N // 16], U16, name="offsets")
+        nc.sync.dma_start(offsets[:], offs)
 
         gamma = held.tile([P, HEADS], F32, name="gamma")
         nc.scalar.dma_start(gamma[:], bn_gamma.rearrange("h o -> (h o)").partition_broadcast(P))
@@ -112,22 +105,30 @@ def tile_attentiontfidf_b_kernel(tc, emb, tf, df, bn_gamma, fc_w, fc_b, offs, ou
             tc.tile_pool(name="work", bufs=4) as work,
             tc.tile_pool(name="heads", bufs=HEADS) as heads,
             tc.tile_pool(name="rounded", bufs=HEADS * DOCS) as rounded,
-            tc.psum_pool(name="ps_gram", bufs=5) as ps_gram,
+            tc.psum_pool(name="ps_gram", bufs=4) as ps_gram,
+            tc.psum_pool(name="ps_rows", bufs=1) as ps_rows,
             tc.psum_pool(name="ps_turn", bufs=2) as ps_turn,
             tc.psum_pool(name="ps_prep", bufs=1) as ps_prep,
         ):
             hsum_ps = ps_prep.tile([P, HEADS * DOCS * T], F32, name="hsum_ps")
-            spread = tables.tile([P, DOCS, L // C, C], F32, name="spread", offset=TABLE_BYTES)
+            counts_ps = ps_gram.tile([P, P], F32, name="counts_ps", tag="gram_ps")
+            nc.tensor.transpose(counts_ps[:], counts[:], ident_f[:])
+            ln_tf = held.tile([P, C], F32, name="ln_tf")
+            ln_df = held.tile([P, C], F32, name="ln_df")
+            nc.scalar.activation(ln_df[:], counts_ps[:, DF_AT:DF_AT + C], ACT.Ln, bias=2.0)
+            nc.scalar.activation(ln_tf[:], counts_ps[:, 0:C], ACT.Ln, bias=1.0)
+            inv_ln_df = held.tile([P, C], F32, name="inv_ln_df")
+            nc.vector.reciprocal(inv_ln_df[:], ln_df[:])
+            wt_c = held.tile([P, C], F32, name="wt_c")
+            nc.vector.tensor_mul(wt_c[:], ln_tf[:], inv_ln_df[:])
             wt = [weights.tile([P, L], F32, name=f"wt{b}") for b in range(DOCS)]
             for b in range(DOCS):
-                nc.vector.tensor_tensor(
-                    spread[:, b],
-                    wt_c[:].unsqueeze(1).to_broadcast([P, L // C, C]),
-                    ident_f[:, b * (L // C):(b + 1) * (L // C)].unsqueeze(2).to_broadcast([P, L // C, C]),
-                    ALU.mult,
-                )
                 wt_ps = ps_gram.tile([P, L], F32, name="wt_ps", tag="gram_ps")
-                nc.tensor.matmul(wt_ps[:], ones[:], spread[:, b].rearrange("p q c -> p (q c)"), start=True, stop=True)
+                for t in range(T):
+                    c = b * T + t
+                    nc.tensor.transpose(
+                        wt_ps[:, t * P:(t + 1) * P], wt_c[:, c:c + 1].to_broadcast([P, P]), ident_f[:]
+                    )
                 nc.scalar.activation(wt[b][:], wt_ps[:], ACT.Copy)
 
             def look_up(a, b, table):
@@ -172,7 +173,7 @@ def tile_attentiontfidf_b_kernel(tc, emb, tf, df, bn_gamma, fc_w, fc_b, offs, ou
                 nc.vector.tensor_tensor(by_block(rest1[:]), by_block(mine), part(0), ALU.subtract)
                 nc.vector.tensor_copy(part(1), by_block(rest1[:]))
                 nc.vector.tensor_tensor(part(2), by_block(rest1[:]), part(1), ALU.subtract)
-                rows_ps = ps_gram.tile([P, L], F32, name="rows_ps", tag="gram_ps")
+                rows_ps = ps_rows.tile([P, L], F32, name="rows_ps")
                 for t in range(T):
                     nc.tensor.matmul(rows_ps[:, t * P:(t + 1) * P], parts[a][:, t, :], ident_bf[:], start=True, stop=True)
                 rows = heads.tile([P, L], BF16, name="rows")
@@ -203,15 +204,21 @@ def tile_attentiontfidf_b_kernel(tc, emb, tf, df, bn_gamma, fc_w, fc_b, offs, ou
                         accum_out=(sum_once if diagonal else sum_twice)[:, column:column + 1],
                     )
 
+            units = [(a, b) for a in range(HEADS) for b in range(DOCS)]
             hb, rows = {}, {}
-            for a in range(HEADS):
-                table = tables.tile([P, S], F32, name=f"table{a}", offset=(a % 2) * TABLE_BYTES)
-                nc.sync.dma_start(table[:], emb[a * P:(a + 1) * P, :])
-                for b in range(DOCS):
+            for step in range(len(units) + LEAD):
+                if step < len(units):
+                    a, b = units[step]
+                    if b == 0:
+                        table = tables.tile([P, S], F32, name=f"table{a}", offset=(a % 2) * TABLE_BYTES)
+                        nc.sync.dma_start(table[:], emb[a * P:(a + 1) * P, :])
                     hb[a, b] = look_up(a, b, table)
-                rows[a] = rows_of_squares(a)
-            for a in range(HEADS):
-                for b in range(DOCS):
+                if step >= LEAD - 1 and (step - LEAD + 1) % DOCS == 0:
+                    a = (step - LEAD + 1) // DOCS
+                    if a < HEADS:
+                        rows[a] = rows_of_squares(a)
+                if step >= LEAD:
+                    a, b = units[step - LEAD]
                     distances(a, b, hb[a, b], rows[a])
             hsum = held.tile([P, HEADS * DOCS], F32, name="hsum")
             nc.vector.tensor_reduce(hsum[:], hsum_ps[:].rearrange("p (c t) -> p c t", t=T), AX.X, ALU.add)

@@ -19,9 +19,8 @@ TABLE_BYTES = 4 * S
 PAIRS = DOCS * L * L
 EPS_BN, TINY = 1e-5, 1e-12
 KEYW = 144
-LEAD = 2 * DOCS
+LEAD = 2
 BANK = 512
-PARTS = 3
 
 FIRST = [t * P for t in range(T)]
 WIDTH = [L - first for first in FIRST]
@@ -88,25 +87,12 @@ def tile_attentiontfidf_b_kernel(tc, emb, tf, df, bn_gamma, fc_w, fc_b, offs, ou
         sqcol = held.tile([P, HEADS * DOCS * T], F32, name="sqcol")
         hsum_sq = held.tile([P, HEADS * DOCS], F32, name="hsum_sq")
 
-        parts = [held.tile([P, T, P], BF16, name=f"parts{a}") for a in range(HEADS)]
-        for a in range(HEADS):
-            nc.gpsimd.memset(parts[a][:], 0.0)
-        chosen_rows = held.tile([P, DOCS], F32, name="chosen_rows")
-        nc.vector.tensor_reduce(
-            chosen_rows[:], ident_f[:, 0:PARTS * DOCS].rearrange("p (r b) -> p b r", b=DOCS), AX.X, ALU.add
-        )
-        choose = [held.tile([P, P], BF16, name=f"choose{b}") for b in range(DOCS)]
-        for b in range(DOCS):
-            nc.vector.tensor_scalar_mul(choose[b][:], ones[:], chosen_rows[:, b:b + 1])
-
         with (
             tc.tile_pool(name="weights", bufs=1) as weights,
             tc.tile_pool(name="tables", bufs=1) as tables,
             tc.tile_pool(name="work", bufs=4) as work,
-            tc.tile_pool(name="heads", bufs=HEADS) as heads,
             tc.tile_pool(name="rounded", bufs=HEADS * DOCS) as rounded,
-            tc.psum_pool(name="ps_gram", bufs=4) as ps_gram,
-            tc.psum_pool(name="ps_rows", bufs=1) as ps_rows,
+            tc.psum_pool(name="ps_gram", bufs=5) as ps_gram,
             tc.psum_pool(name="ps_turn", bufs=2) as ps_turn,
             tc.psum_pool(name="ps_prep", bufs=1) as ps_prep,
         ):
@@ -150,6 +136,7 @@ def tile_attentiontfidf_b_kernel(tc, emb, tf, df, bn_gamma, fc_w, fc_b, offs, ou
                     nc.scalar.activation(
                         squares[:], hT_ps[:, t, :], ACT.Square, accum_out=sq[:, block + t:block + t + 1]
                     )
+                nc.scalar.activation(sqcol[:, block:block + T], sq[:, block:block + T], ACT.Copy, scale=-0.5)
                 nc.scalar.activation(keys[:, block:block + T, 0:P], hT_ps[:], ACT.Copy)
                 for t in range(T):
                     nc.tensor.matmul(
@@ -157,39 +144,21 @@ def tile_attentiontfidf_b_kernel(tc, emb, tf, df, bn_gamma, fc_w, fc_b, offs, ou
                     )
                 return hb
 
-            def rows_of_squares(a):
-                first = a * DOCS * T
-                mine = sqcol[:, first:first + DOCS * T]
-                nc.vector.tensor_scalar_mul(mine, sq[:, first:first + DOCS * T], -0.5)
-
-                def part(r):
-                    return parts[a][:, :, r * DOCS:(r + 1) * DOCS]
-
-                def by_block(columns):
-                    return columns.rearrange("p (b t) -> p t b", t=T)
-
-                rest1 = heads.tile([P, DOCS * T], F32, name="rest1")
-                nc.vector.tensor_copy(part(0), by_block(mine))
-                nc.vector.tensor_tensor(by_block(rest1[:]), by_block(mine), part(0), ALU.subtract)
-                nc.vector.tensor_copy(part(1), by_block(rest1[:]))
-                nc.vector.tensor_tensor(part(2), by_block(rest1[:]), part(1), ALU.subtract)
-                rows_ps = ps_rows.tile([P, L], F32, name="rows_ps")
-                for t in range(T):
-                    nc.tensor.matmul(rows_ps[:, t * P:(t + 1) * P], parts[a][:, t, :], ident_bf[:], start=True, stop=True)
-                rows = heads.tile([P, L], BF16, name="rows")
-                nc.scalar.activation(rows[:], rows_ps[:], ACT.Copy)
-                return rows
-
-            def distances(a, b, hb, rows):
+            def distances(a, b, hb):
                 block = (a * DOCS + b) * T
                 for t in ROW_ORDER:
                     gram_ps = ps_gram.tile([P, L], F32, name="gram_ps")
                     for offset, first, count in pieces(t):
-                        group = gram_ps[:, offset:offset + count * P]
-                        nc.tensor.matmul(group, choose[b][:], rows[:, first * P:(first + count) * P], start=True, stop=False)
                         nc.tensor.matmul(
-                            group, hb[:, t * P:(t + 1) * P], hb[:, first * P:(first + count) * P], start=False, stop=True
+                            gram_ps[:, offset:offset + count * P],
+                            hb[:, t * P:(t + 1) * P], hb[:, first * P:(first + count) * P], start=True, stop=False,
                         )
+                        for s in range(count):
+                            nc.tensor.matmul(
+                                gram_ps[:, offset + s * P:offset + (s + 1) * P],
+                                sqcol[:, block + first + s:block + first + s + 1].to_broadcast([P, P]), ident_f[:],
+                                start=False, stop=(s == count - 1), is_transpose=True,
+                            )
                     nc.vector.tensor_scalar(
                         dist[a][b][:, START[t]:START[t] + WIDTH[t]], gram_ps[:, 0:WIDTH[t]],
                         sqcol[:, block + t:block + t + 1], 0.0, ALU.add, ALU.min,
@@ -205,7 +174,7 @@ def tile_attentiontfidf_b_kernel(tc, emb, tf, df, bn_gamma, fc_w, fc_b, offs, ou
                     )
 
             units = [(a, b) for a in range(HEADS) for b in range(DOCS)]
-            hb, rows = {}, {}
+            hb = {}
             for step in range(len(units) + LEAD):
                 if step < len(units):
                     a, b = units[step]
@@ -213,13 +182,9 @@ def tile_attentiontfidf_b_kernel(tc, emb, tf, df, bn_gamma, fc_w, fc_b, offs, ou
                         table = tables.tile([P, S], F32, name=f"table{a}", offset=(a % 2) * TABLE_BYTES)
                         nc.sync.dma_start(table[:], emb[a * P:(a + 1) * P, :])
                     hb[a, b] = look_up(a, b, table)
-                if step >= LEAD - 1 and (step - LEAD + 1) % DOCS == 0:
-                    a = (step - LEAD + 1) // DOCS
-                    if a < HEADS:
-                        rows[a] = rows_of_squares(a)
                 if step >= LEAD:
                     a, b = units[step - LEAD]
-                    distances(a, b, hb[a, b], rows[a])
+                    distances(a, b, hb[a, b])
             hsum = held.tile([P, HEADS * DOCS], F32, name="hsum")
             nc.vector.tensor_reduce(hsum[:], hsum_ps[:].rearrange("p (c t) -> p c t", t=T), AX.X, ALU.add)
             nc.vector.tensor_mul(hsum_sq[:], hsum[:], hsum[:])

@@ -14,7 +14,7 @@ T = L // P
 S = 4096
 N = DOCS * L
 C = N // P
-DF_AT = 32
+DF_AT = 2 * C
 TABLE_BYTES = 4 * S
 PAIRS = DOCS * L * L
 EPS_BN, TINY = 1e-5, 1e-12
@@ -55,7 +55,21 @@ def tile_attentiontfidf_b_kernel(tc, emb, tf, df, bn_gamma, fc_w, fc_b, offs, ou
     with (
         tc.tile_pool(name="held", bufs=1) as held,
         tc.tile_pool(name="dists", bufs=1) as dists,
+        tc.tile_pool(name="tables", bufs=1) as tables,
     ):
+        def load_table(a):
+            table = tables.tile([P, S], F32, name=f"table{a}", offset=(a % 2) * TABLE_BYTES)
+            nc.sync.dma_start(table[:], emb[a * P:(a + 1) * P, :])
+            return table
+
+        counts = held.tile([2 * DF_AT, P], F32, name="counts")
+        for row in (0, C):
+            nc.sync.dma_start(counts[row:row + C, :], tf.rearrange("o (c p) -> (o c) p", p=P))
+            nc.scalar.dma_start(counts[DF_AT + row:DF_AT + row + C, :], df.rearrange("o (c p) -> (o c) p", p=P))
+        offsets = held.tile([P, N // 16], U16, name="offsets")
+        nc.sync.dma_start(offsets[:], offs)
+        table = load_table(0)
+
         ident_f = held.tile([P, P], F32, name="ident_f")
         make_identity(nc, ident_f[:])
         ones = held.tile([P, P], F32, name="ones")
@@ -65,19 +79,12 @@ def tile_attentiontfidf_b_kernel(tc, emb, tf, df, bn_gamma, fc_w, fc_b, offs, ou
         ident_bf = held.tile([P, P], BF16, name="ident_bf")
         nc.vector.tensor_copy(ident_bf[:], ident_f[:])
 
-        counts = held.tile([P, P], F32, name="counts")
-        nc.vector.memset(counts[:], 0.0)
-        nc.sync.dma_start(counts[0:C, :], tf.rearrange("o (c p) -> (o c) p", p=P))
-        nc.scalar.dma_start(counts[DF_AT:DF_AT + C, :], df.rearrange("o (c p) -> (o c) p", p=P))
-        offsets = held.tile([P, N // 16], U16, name="offsets")
-        nc.sync.dma_start(offsets[:], offs)
-
         gamma = held.tile([P, HEADS], F32, name="gamma")
-        nc.scalar.dma_start(gamma[:], bn_gamma.rearrange("h o -> (h o)").partition_broadcast(P))
+        nc.sync.dma_start(gamma[:], bn_gamma.rearrange("h o -> (h o)").partition_broadcast(P))
         fcw = held.tile([P, HEADS, P], BF16, name="fcw")
-        nc.scalar.dma_start(fcw[:], fc_w.rearrange("(a k) m -> k a m", k=P))
+        nc.sync.dma_start(fcw[:], fc_w.rearrange("(a k) m -> k a m", k=P))
         fcb = held.tile([P, 1], F32, name="fcb")
-        nc.scalar.dma_start(fcb[:], fc_b)
+        nc.sync.dma_start(fcb[:], fc_b)
 
         keys = held.tile([P, HEADS * DOCS * T, KEYW], BF16, name="keys")
         dist = [[dists.tile([P, KEPT], F32, name=f"dist{a}{b}") for b in range(DOCS)] for a in range(HEADS)]
@@ -89,7 +96,6 @@ def tile_attentiontfidf_b_kernel(tc, emb, tf, df, bn_gamma, fc_w, fc_b, offs, ou
 
         with (
             tc.tile_pool(name="weights", bufs=1) as weights,
-            tc.tile_pool(name="tables", bufs=1) as tables,
             tc.tile_pool(name="work", bufs=4) as work,
             tc.tile_pool(name="rounded", bufs=HEADS * DOCS) as rounded,
             tc.psum_pool(name="ps_gram", bufs=5) as ps_gram,
@@ -97,8 +103,8 @@ def tile_attentiontfidf_b_kernel(tc, emb, tf, df, bn_gamma, fc_w, fc_b, offs, ou
             tc.psum_pool(name="ps_prep", bufs=1) as ps_prep,
         ):
             hsum_ps = ps_prep.tile([P, HEADS * DOCS * T], F32, name="hsum_ps")
-            counts_ps = ps_gram.tile([P, P], F32, name="counts_ps", tag="gram_ps")
-            nc.tensor.transpose(counts_ps[:], counts[:], ident_f[:])
+            counts_ps = ps_gram.tile([P, 2 * DF_AT], F32, name="counts_ps", tag="gram_ps")
+            nc.tensor.transpose(counts_ps[:], counts[:], ident_f[0:2 * DF_AT, 0:2 * DF_AT])
             ln_tf = held.tile([P, C], F32, name="ln_tf")
             ln_df = held.tile([P, C], F32, name="ln_df")
             nc.scalar.activation(ln_df[:], counts_ps[:, DF_AT:DF_AT + C], ACT.Ln, bias=2.0)
@@ -178,9 +184,8 @@ def tile_attentiontfidf_b_kernel(tc, emb, tf, df, bn_gamma, fc_w, fc_b, offs, ou
             for step in range(len(units) + LEAD):
                 if step < len(units):
                     a, b = units[step]
-                    if b == 0:
-                        table = tables.tile([P, S], F32, name=f"table{a}", offset=(a % 2) * TABLE_BYTES)
-                        nc.sync.dma_start(table[:], emb[a * P:(a + 1) * P, :])
+                    if b == 0 and a > 0:
+                        table = load_table(a)
                     hb[a, b] = look_up(a, b, table)
                 if step >= LEAD:
                     a, b = units[step - LEAD]
@@ -226,7 +231,7 @@ def tile_attentiontfidf_b_kernel(tc, emb, tf, df, bn_gamma, fc_w, fc_b, offs, ou
         with (
             tc.tile_pool(name="exps", bufs=4) as exps,
             tc.tile_pool(name="small", bufs=4) as small,
-            tc.tile_pool(name="vos", bufs=2 * HEADS) as vos,
+            tc.tile_pool(name="vos", bufs=4) as vos,
             tc.tile_pool(name="outs", bufs=2) as outs,
             tc.psum_pool(name="ps_v", bufs=3) as ps_v,
             tc.psum_pool(name="ps_t", bufs=2) as ps_t,
@@ -296,18 +301,31 @@ def tile_attentiontfidf_b_kernel(tc, emb, tf, df, bn_gamma, fc_w, fc_b, offs, ou
                 nc.vector.tensor_copy(vo_a[:], vo_ps[:])
                 return vo_a
 
-            def class_scores(b, vo):
-                lg_ps = ps_o.tile([P, L], F32, name="lg_ps")
-                for a in range(HEADS):
-                    nc.tensor.matmul(lg_ps[:], fcw[:, a, :], vo[a][:], start=(a == 0), stop=(a == HEADS - 1))
-                lg = outs.tile([P, L], F32, name="lg")
-                nc.vector.tensor_scalar_add(lg[:], lg_ps[:], fcb[:, 0:1])
-                nc.sync.dma_start(out[0:P, b * L:(b + 1) * L], lg[:])
+            lg_ps = {}
+
+            def class_scores(a, b, vo_a):
+                if a == 0:
+                    lg_ps[b] = ps_o.tile([P, L], F32, name="lg_ps")
+                nc.tensor.matmul(lg_ps[b][:], fcw[:, a, :], vo_a[:], start=(a == 0), stop=(a == HEADS - 1))
+                if a == HEADS - 1:
+                    lg = outs.tile([P, L], F32, name="lg")
+                    nc.vector.tensor_scalar_add(lg[:], lg_ps[b][:], fcb[:, 0:1])
+                    nc.sync.dma_start(out[0:P, b * L:(b + 1) * L], lg[:])
+
+            def last_row():
+                received_sum = small.tile([P, DOCS * T], F32, name="received_sum")
+                nc.vector.tensor_reduce(
+                    received_sum[:], received[:].rearrange("p (a c) -> p c a", a=HEADS), AX.X, ALU.add
+                )
+                ws_ps = ps_t.tile([P, P], F32, name="ws_ps", tag="vo_ps")
+                nc.tensor.transpose(ws_ps[0:DOCS * T, :], received_sum[:], ident_f[:])
+                ws = outs.tile([DOCS * T, P], F32, name="ws")
+                nc.vector.tensor_scalar_mul(ws[:], ws_ps[0:DOCS * T, :], 1.0 / HEADS)
+                nc.sync.dma_start(out[P:P + 1, :].rearrange("o (c p) -> (o c) p", p=P), ws[:])
 
             units = [(a, b) for b in range(DOCS) for a in range(HEADS)]
-            e_of, sums_of, rinv_of, voT_of = {}, {}, {}, {}
-            vo = [[] for b in range(DOCS)]
-            for step in range(len(units) + 3):
+            e_of, sums_of, rinv_of, voT_of, vo_of = {}, {}, {}, {}, {}
+            for step in range(len(units) + 4):
                 if step < len(units):
                     a, b = units[step]
                     e_of[step], *sums_of[step] = exponentials(a, b)
@@ -317,18 +335,11 @@ def tile_attentiontfidf_b_kernel(tc, emb, tf, df, bn_gamma, fc_w, fc_b, offs, ou
                 if 0 <= step - 2 < len(units):
                     a, b = units[step - 2]
                     voT_of[step - 2] = weighted_sums(a, b, e_of[step - 2], rinv_of[step - 2])
+                if step - 2 == len(units) - 1:
+                    last_row()
                 if 0 <= step - 3 < len(units):
                     a, b = units[step - 3]
-                    vo[b].append(channels_first(voT_of[step - 3]))
-                    if len(vo[b]) == HEADS:
-                        class_scores(b, vo[b])
-
-            received_sum = small.tile([P, DOCS * T], F32, name="received_sum")
-            nc.vector.tensor_reduce(
-                received_sum[:], received[:].rearrange("p (a c) -> p c a", a=HEADS), AX.X, ALU.add
-            )
-            ws_ps = ps_o.tile([P, P], F32, name="ws_ps", tag="lg_ps")
-            nc.tensor.transpose(ws_ps[0:DOCS * T, :], received_sum[:], ident_f[:])
-            ws = outs.tile([DOCS * T, P], F32, name="ws")
-            nc.vector.tensor_scalar_mul(ws[:], ws_ps[0:DOCS * T, :], 1.0 / HEADS)
-            nc.sync.dma_start(out[P:P + 1, :].rearrange("o (c p) -> (o c) p", p=P), ws[:])
+                    vo_of[step - 3] = channels_first(voT_of[step - 3])
+                if 0 <= step - 4 < len(units):
+                    a, b = units[step - 4]
+                    class_scores(a, b, vo_of[step - 4])

@@ -15,7 +15,6 @@ S = 4096
 N = DOCS * L
 C = N // P
 DF_AT = 2 * C
-TABLE_BYTES = 4 * S
 PAIRS = DOCS * L * L
 EPS_BN, TINY = 1e-5, 1e-12
 KEYW = 144
@@ -58,7 +57,7 @@ def tile_attentiontfidf_b_kernel(tc, emb, tf, df, bn_gamma, fc_w, fc_b, offs, ou
         tc.tile_pool(name="tables", bufs=1) as tables,
     ):
         def load_table(a):
-            table = tables.tile([P, S], F32, name=f"table{a}", offset=(a % 2) * TABLE_BYTES)
+            table = tables.tile([P, S], F32, name=f"table{a}")
             nc.sync.dma_start(table[:], emb[a * P:(a + 1) * P, :])
             return table
 
@@ -72,8 +71,10 @@ def tile_attentiontfidf_b_kernel(tc, emb, tf, df, bn_gamma, fc_w, fc_b, offs, ou
 
         ident_f = held.tile([P, P], F32, name="ident_f")
         make_identity(nc, ident_f[:])
-        ones = held.tile([P, P], F32, name="ones")
-        nc.vector.memset(ones[:], 1.0)
+        share = held.tile([P, P], F32, name="share")
+        nc.vector.memset(share[:], 1.0 / PAIRS)
+        minus_half = held.tile([P, HEADS], F32, name="minus_half")
+        nc.vector.memset(minus_half[:], -0.5)
         one_bf = held.tile([P, 1], BF16, name="one_bf")
         nc.vector.memset(one_bf[:], 1.0)
         ident_bf = held.tile([P, P], BF16, name="ident_bf")
@@ -92,7 +93,7 @@ def tile_attentiontfidf_b_kernel(tc, emb, tf, df, bn_gamma, fc_w, fc_b, offs, ou
         sum_twice = held.tile([P, HEADS * DOCS * 2], F32, name="sum_twice")
         sq = held.tile([P, HEADS * DOCS * T], F32, name="sq")
         sqcol = held.tile([P, HEADS * DOCS * T], F32, name="sqcol")
-        hsum_sq = held.tile([P, HEADS * DOCS], F32, name="hsum_sq")
+        gain, shift = {}, {}
 
         with (
             tc.tile_pool(name="weights", bufs=1) as weights,
@@ -133,7 +134,10 @@ def tile_attentiontfidf_b_kernel(tc, emb, tf, df, bn_gamma, fc_w, fc_b, offs, ou
                     ALU.mult,
                 )
                 hb = rounded.tile([P, L], BF16, name="hb")
-                nc.vector.tensor_copy(hb[:], h[:])
+                if b == DOCS - 1:
+                    nc.scalar.copy(hb[:], h[:])
+                else:
+                    nc.vector.tensor_copy(hb[:], h[:])
                 hT_ps = ps_turn.tile([P, T, P], F32, name="hT_ps")
                 for t in range(T):
                     nc.tensor.transpose(hT_ps[:, t, :], h[:, t * P:(t + 1) * P], ident_f[:])
@@ -179,6 +183,50 @@ def tile_attentiontfidf_b_kernel(tc, emb, tf, df, bn_gamma, fc_w, fc_b, offs, ou
                         accum_out=(sum_once if diagonal else sum_twice)[:, column:column + 1],
                     )
 
+            def statistics(heads):
+                first, count = heads[0], len(heads)
+
+                def mine(columns, each):
+                    return columns[:, first * each:(first + count) * each]
+
+                def per_head(out, columns):
+                    nc.vector.tensor_reduce(out, columns.rearrange("p (a c) -> p a c", a=count), AX.X, ALU.add)
+
+                def column(name, width=count):
+                    return held.tile([P, width], F32, name=f"{name}{first}")
+
+                hsum, hsum_sq = column("hsum", count * DOCS), column("hsum_sq", count * DOCS)
+                nc.vector.tensor_reduce(
+                    hsum[:], mine(hsum_ps, DOCS * T).rearrange("p (c t) -> p c t", t=T), AX.X, ALU.add
+                )
+                nc.vector.tensor_mul(hsum_sq[:], hsum[:], hsum[:])
+                sum_hsum_sq, sum_sqcol = column("sum_hsum_sq"), column("sum_sqcol")
+                per_head(sum_hsum_sq[:], hsum_sq[:])
+                per_head(sum_sqcol[:], mine(sqcol, DOCS * T))
+                runs = 2 * DOCS * count
+                sums = column("sums", runs + count)
+                nc.vector.scalar_tensor_tensor(
+                    sums[:, runs:runs + count], sum_sqcol[:], 2.0 * L, sum_hsum_sq[:], ALU.mult, ALU.add
+                )
+                nc.vector.scalar_tensor_tensor(
+                    sums[:, 0:runs], mine(sum_twice, 2 * DOCS), 2.0, mine(sum_once, 2 * DOCS), ALU.mult, ALU.add
+                )
+                mean_ps = ps_turn.tile([P, runs + count], F32, name="mean_ps", tag="hT_ps")
+                nc.tensor.matmul(mean_ps[:], share[:], sums[:], start=True, stop=True)
+                mean, mean_sq_eps, sq_mean, var_eps = column("mean"), column("mean_sq_eps"), column("sq_mean"), column("var_eps")
+                per_head(mean[:], mean_ps[:, 0:runs])
+                nc.vector.tensor_scalar(
+                    mean_sq_eps[:], mean_ps[:, runs:runs + count], -2.0, TINY + EPS_BN, ALU.mult, ALU.add
+                )
+                nc.vector.tensor_mul(sq_mean[:], mean[:], mean[:])
+                nc.vector.tensor_sub(var_eps[:], mean_sq_eps[:], sq_mean[:])
+                inv_sd, gains, shifts = column("inv_sd"), column("gains"), column("shifts")
+                nc.gpsimd.tensor_tensor(inv_sd[:], var_eps[:], minus_half[:, 0:count], ALU.pow)
+                nc.vector.tensor_mul(gains[:], gamma[:, first:first + count], inv_sd[:])
+                nc.vector.scalar_tensor_tensor(shifts[:], mean[:], -1.0, gains[:], ALU.mult, ALU.mult)
+                for i, a in enumerate(heads):
+                    gain[a], shift[a] = gains[:, i:i + 1], shifts[:, i:i + 1]
+
             units = [(a, b) for a in range(HEADS) for b in range(DOCS)]
             hb = {}
             for step in range(len(units) + LEAD):
@@ -187,45 +235,12 @@ def tile_attentiontfidf_b_kernel(tc, emb, tf, df, bn_gamma, fc_w, fc_b, offs, ou
                     if b == 0 and a > 0:
                         table = load_table(a)
                     hb[a, b] = look_up(a, b, table)
+                if step == len(units):
+                    statistics(range(HEADS - 1))
                 if step >= LEAD:
                     a, b = units[step - LEAD]
                     distances(a, b, hb[a, b])
-            hsum = held.tile([P, HEADS * DOCS], F32, name="hsum")
-            nc.vector.tensor_reduce(hsum[:], hsum_ps[:].rearrange("p (c t) -> p c t", t=T), AX.X, ALU.add)
-            nc.vector.tensor_mul(hsum_sq[:], hsum[:], hsum[:])
-
-        gain = held.tile([P, HEADS], F32, name="gain")
-        shift = held.tile([P, HEADS], F32, name="shift")
-        with tc.psum_pool(name="ps_stat", bufs=1) as ps_stat:
-            sums = held.tile([P, 2 * HEADS], F32, name="sums")
-            once = held.tile([P, HEADS], F32, name="once")
-            nc.vector.tensor_reduce(once[:], sum_once[:].rearrange("p (a c) -> p a c", a=HEADS), AX.X, ALU.add)
-            twice = held.tile([P, HEADS], F32, name="twice")
-            nc.vector.tensor_reduce(twice[:], sum_twice[:].rearrange("p (a c) -> p a c", a=HEADS), AX.X, ALU.add)
-            nc.vector.scalar_tensor_tensor(sums[:, 0:HEADS], twice[:], 2.0, once[:], ALU.mult, ALU.add)
-            sum_hsum_sq = held.tile([P, HEADS], F32, name="sum_hsum_sq")
-            nc.vector.tensor_reduce(sum_hsum_sq[:], hsum_sq[:].rearrange("p (a c) -> p a c", a=HEADS), AX.X, ALU.add)
-            sum_sqcol = held.tile([P, HEADS], F32, name="sum_sqcol")
-            nc.vector.tensor_reduce(sum_sqcol[:], sqcol[:].rearrange("p (a c) -> p a c", a=HEADS), AX.X, ALU.add)
-            nc.vector.scalar_tensor_tensor(
-                sums[:, HEADS:2 * HEADS], sum_sqcol[:], 2.0 * L, sum_hsum_sq[:], ALU.mult, ALU.add
-            )
-            total_ps = ps_stat.tile([P, 2 * HEADS], F32, name="total_ps")
-            nc.tensor.matmul(total_ps[:], ones[:], sums[:], start=True, stop=True)
-            mean = held.tile([P, HEADS], F32, name="mean")
-            nc.vector.tensor_scalar_mul(mean[:], total_ps[:, 0:HEADS], 1.0 / PAIRS)
-            mean_sq = held.tile([P, HEADS], F32, name="mean_sq")
-            nc.vector.tensor_scalar(mean_sq[:], total_ps[:, HEADS:2 * HEADS], -2.0 / PAIRS, TINY, ALU.mult, ALU.add)
-            sq_mean = held.tile([P, HEADS], F32, name="sq_mean")
-            nc.vector.tensor_mul(sq_mean[:], mean[:], mean[:])
-            var_eps = held.tile([P, HEADS], F32, name="var_eps")
-            nc.vector.scalar_tensor_tensor(var_eps[:], mean_sq[:], EPS_BN, sq_mean[:], ALU.add, ALU.subtract)
-            sd = held.tile([P, HEADS], F32, name="sd")
-            nc.scalar.activation(sd[:], var_eps[:], ACT.Sqrt)
-            inv_sd = held.tile([P, HEADS], F32, name="inv_sd")
-            nc.vector.reciprocal(inv_sd[:], sd[:])
-            nc.vector.tensor_mul(gain[:], gamma[:], inv_sd[:])
-            nc.vector.scalar_tensor_tensor(shift[:], mean[:], -1.0, gain[:], ALU.mult, ALU.mult)
+            statistics([HEADS - 1])
 
         received = held.tile([P, HEADS * DOCS * T], F32, name="received")
         with (
@@ -234,9 +249,9 @@ def tile_attentiontfidf_b_kernel(tc, emb, tf, df, bn_gamma, fc_w, fc_b, offs, ou
             tc.tile_pool(name="vos", bufs=4) as vos,
             tc.tile_pool(name="outs", bufs=2) as outs,
             tc.psum_pool(name="ps_v", bufs=3) as ps_v,
+            tc.psum_pool(name="ps_e", bufs=2) as ps_e,
             tc.psum_pool(name="ps_t", bufs=2) as ps_t,
             tc.psum_pool(name="ps_o", bufs=1) as ps_o,
-            tc.psum_pool(name="ps_e", bufs=2) as ps_e,
         ):
             def block_of(e, t, s):
                 begin = s * P if s < t else FIRST[t] + kept_at(t, s)
@@ -249,7 +264,7 @@ def tile_attentiontfidf_b_kernel(tc, emb, tf, df, bn_gamma, fc_w, fc_b, offs, ou
                 for t in range(T):
                     nc.scalar.activation(
                         e[:, t, FIRST[t]:L], dist[a][b][:, START[t]:START[t] + WIDTH[t]], ACT.Exp,
-                        bias=shift[:, a:a + 1], scale=gain[:, a:a + 1],
+                        bias=shift[a], scale=gain[a],
                         accum_out=(rowsum if t == 0 else right_sum)[:, t:t + 1],
                     )
                 return e, right_sum, rowsum

@@ -18,31 +18,23 @@ DF_AT = 2 * C
 PAIRS = DOCS * L * L
 EPS_BN, TINY = 1e-5, 1e-12
 KEYW = 144
-LEAD = 2
+LEAD = 3
 BANK = 512
 
 FIRST = [t * P for t in range(T)]
 WIDTH = [L - first for first in FIRST]
 KEPT = sum(WIDTH)
-ROW_ORDER = [3, 0, 1, 2]
-DIAGONAL_LAST = [t == 1 for t in range(T)]
-START = [sum(WIDTH[r] for r in ROW_ORDER[:ROW_ORDER.index(t)]) for t in range(T)]
-RUNS = [(0, 2 * P, True), (2 * P, 5 * P, False), (7 * P, 2 * P, True), (9 * P, P, False)]
+SLOT = [3, 2, 1, 0]
+STEP = [2, 2, 7, 1]
+RUNS = [(T * P, KEPT - T * P), (0, T * P)]
 BELOW = [sum(FIRST[:t]) for t in range(T)]
 MIRRORED = sum(FIRST)
 
 
-def pieces(t):
-    if DIAGONAL_LAST[t]:
-        return [(0, t + 1, T - t - 1), ((T - t - 1) * P, t, 1)]
-    return [(0, t, T - t)]
-
-
-def kept_at(t, s):
-    for offset, first, count in pieces(t):
-        if first <= s < first + count:
-            return offset + (s - first) * P
-    raise ValueError("not kept")
+def row_block(dist_tile, t):
+    count = T - t
+    blocks = dist_tile[:].rearrange("p (s c) -> p s c", c=P)
+    return blocks[:, SLOT[t]:SLOT[t] + STEP[t] * (count - 1) + 1:STEP[t], :]
 
 
 FLOPS = 2 * (2 * HEADS * DOCS * L * L * P) + 2 * (HEADS * P) * P * N
@@ -89,8 +81,8 @@ def tile_attentiontfidf_b_kernel(tc, emb, tf, df, bn_gamma, fc_w, fc_b, offs, ou
 
         keys = held.tile([P, HEADS * DOCS * T, KEYW], BF16, name="keys")
         dist = [[dists.tile([P, KEPT], F32, name=f"dist{a}{b}") for b in range(DOCS)] for a in range(HEADS)]
-        sum_once = held.tile([P, HEADS * DOCS * 2], F32, name="sum_once")
-        sum_twice = held.tile([P, HEADS * DOCS * 2], F32, name="sum_twice")
+        sum_once = held.tile([P, HEADS * DOCS], F32, name="sum_once")
+        sum_twice = held.tile([P, HEADS * DOCS], F32, name="sum_twice")
         sq = held.tile([P, HEADS * DOCS * T], F32, name="sq")
         sqcol = held.tile([P, HEADS * DOCS * T], F32, name="sqcol")
         gain, shift = {}, {}
@@ -156,31 +148,25 @@ def tile_attentiontfidf_b_kernel(tc, emb, tf, df, bn_gamma, fc_w, fc_b, offs, ou
 
             def distances(a, b, hb):
                 block = (a * DOCS + b) * T
-                for t in ROW_ORDER:
+                for t in range(T):
                     gram_ps = ps_gram.tile([P, L], F32, name="gram_ps")
-                    for offset, first, count in pieces(t):
+                    width = WIDTH[t]
+                    nc.tensor.matmul(gram_ps[:, 0:width], hb[:, t * P:(t + 1) * P], hb[:, t * P:L], start=True, stop=False)
+                    for s in range(t, T):
                         nc.tensor.matmul(
-                            gram_ps[:, offset:offset + count * P],
-                            hb[:, t * P:(t + 1) * P], hb[:, first * P:(first + count) * P], start=True, stop=False,
+                            gram_ps[:, (s - t) * P:(s - t + 1) * P],
+                            sqcol[:, block + s:block + s + 1].to_broadcast([P, P]), ident_f[:],
+                            start=False, stop=(s == T - 1), is_transpose=True,
                         )
-                        for s in range(count):
-                            nc.tensor.matmul(
-                                gram_ps[:, offset + s * P:offset + (s + 1) * P],
-                                sqcol[:, block + first + s:block + first + s + 1].to_broadcast([P, P]), ident_f[:],
-                                start=False, stop=(s == count - 1), is_transpose=True,
-                            )
                     nc.vector.tensor_scalar(
-                        dist[a][b][:, START[t]:START[t] + WIDTH[t]], gram_ps[:, 0:WIDTH[t]],
+                        row_block(dist[a][b], t), gram_ps[:, 0:width].rearrange("p (s c) -> p s c", c=P),
                         sqcol[:, block + t:block + t + 1], 0.0, ALU.add, ALU.min,
                     )
-                seen = {True: 0, False: 0}
-                for begin, width, diagonal in RUNS:
-                    column = (a * DOCS + b) * 2 + seen[diagonal]
-                    seen[diagonal] += 1
+                unit = a * DOCS + b
+                for (begin, width), sums in zip(RUNS, (sum_twice, sum_once)):
                     run = dist[a][b][:, begin:begin + width]
                     nc.scalar.activation(
-                        run, run, ACT.Sqrt, scale=-2.0, bias=TINY,
-                        accum_out=(sum_once if diagonal else sum_twice)[:, column:column + 1],
+                        run, run, ACT.Sqrt, scale=-2.0, bias=TINY, accum_out=sums[:, unit:unit + 1],
                     )
 
             def statistics(heads):
@@ -203,20 +189,20 @@ def tile_attentiontfidf_b_kernel(tc, emb, tf, df, bn_gamma, fc_w, fc_b, offs, ou
                 sum_hsum_sq, sum_sqcol = column("sum_hsum_sq"), column("sum_sqcol")
                 per_head(sum_hsum_sq[:], hsum_sq[:])
                 per_head(sum_sqcol[:], mine(sqcol, DOCS * T))
-                runs = 2 * DOCS * count
-                sums = column("sums", runs + count)
+                units_here = DOCS * count
+                sums = column("sums", units_here + count)
                 nc.vector.scalar_tensor_tensor(
-                    sums[:, runs:runs + count], sum_sqcol[:], 2.0 * L, sum_hsum_sq[:], ALU.mult, ALU.add
+                    sums[:, units_here:units_here + count], sum_sqcol[:], 2.0 * L, sum_hsum_sq[:], ALU.mult, ALU.add
                 )
                 nc.vector.scalar_tensor_tensor(
-                    sums[:, 0:runs], mine(sum_twice, 2 * DOCS), 2.0, mine(sum_once, 2 * DOCS), ALU.mult, ALU.add
+                    sums[:, 0:units_here], mine(sum_twice, DOCS), 2.0, mine(sum_once, DOCS), ALU.mult, ALU.add
                 )
-                mean_ps = ps_turn.tile([P, runs + count], F32, name="mean_ps", tag="hT_ps")
+                mean_ps = ps_turn.tile([P, units_here + count], F32, name="mean_ps", tag="hT_ps")
                 nc.tensor.matmul(mean_ps[:], share[:], sums[:], start=True, stop=True)
                 mean, mean_sq_eps, sq_mean, var_eps = column("mean"), column("mean_sq_eps"), column("sq_mean"), column("var_eps")
-                per_head(mean[:], mean_ps[:, 0:runs])
+                per_head(mean[:], mean_ps[:, 0:units_here])
                 nc.vector.tensor_scalar(
-                    mean_sq_eps[:], mean_ps[:, runs:runs + count], -2.0, TINY + EPS_BN, ALU.mult, ALU.add
+                    mean_sq_eps[:], mean_ps[:, units_here:units_here + count], -2.0, TINY + EPS_BN, ALU.mult, ALU.add
                 )
                 nc.vector.tensor_mul(sq_mean[:], mean[:], mean[:])
                 nc.vector.tensor_sub(var_eps[:], mean_sq_eps[:], sq_mean[:])
@@ -254,8 +240,7 @@ def tile_attentiontfidf_b_kernel(tc, emb, tf, df, bn_gamma, fc_w, fc_b, offs, ou
             tc.psum_pool(name="ps_o", bufs=1) as ps_o,
         ):
             def block_of(e, t, s):
-                begin = s * P if s < t else FIRST[t] + kept_at(t, s)
-                return e[:, t, begin:begin + P]
+                return e[:, t, s * P:(s + 1) * P]
 
             def exponentials(a, b):
                 e = exps.tile([P, T, L], BF16, name="e")
@@ -263,7 +248,7 @@ def tile_attentiontfidf_b_kernel(tc, emb, tf, df, bn_gamma, fc_w, fc_b, offs, ou
                 rowsum = small.tile([P, T], F32, name="rowsum")
                 for t in range(T):
                     nc.scalar.activation(
-                        e[:, t, FIRST[t]:L], dist[a][b][:, START[t]:START[t] + WIDTH[t]], ACT.Exp,
+                        e[:, t, FIRST[t]:L].rearrange("p (s c) -> p s c", c=P), row_block(dist[a][b], t), ACT.Exp,
                         bias=shift[a], scale=gain[a],
                         accum_out=(rowsum if t == 0 else right_sum)[:, t:t + 1],
                     )

import concourse.mybir as mybir
from concourse.masks import make_identity

F32 = mybir.dt.float32
BF16 = mybir.dt.bfloat16
U16 = mybir.dt.uint16
ALU = mybir.AluOpType
ACT = mybir.ActivationFunctionType
AX = mybir.AxisListType

P = 128
HEADS, DOCS, L = 4, 4, 512
T = L // P
S = 4096
N = DOCS * L
C = N // P
DF_AT = 2 * C
PAIRS = DOCS * L * L
EPS_BN, TINY = 1e-5, 1e-12
KEYW = 144
LEAD = 3
BANK = 512

FIRST = [t * P for t in range(T)]
WIDTH = [L - first for first in FIRST]
KEPT = sum(WIDTH)
SLOT = [3, 2, 1, 0]
STEP = [2, 2, 7, 1]
RUNS = [(T * P, KEPT - T * P), (0, T * P)]
BELOW = [sum(FIRST[:t]) for t in range(T)]
MIRRORED = sum(FIRST)


def row_block(dist_tile, t):
    count = T - t
    blocks = dist_tile[:].rearrange("p (s c) -> p s c", c=P)
    return blocks[:, SLOT[t]:SLOT[t] + STEP[t] * (count - 1) + 1:STEP[t], :]


FLOPS = 2 * (2 * HEADS * DOCS * L * L * P) + 2 * (HEADS * P) * P * N
BYTES = 4 * HEADS * P * N + 2 * 4 * N + 2 * N + 2 * HEADS * P * P + 4 * (P + 1) * N


def tile_attentiontfidf_b_kernel(tc, emb, tf, df, bn_gamma, fc_w, fc_b, offs, out):
    nc = tc.nc
    with (
        tc.tile_pool(name="held", bufs=1) as held,
        tc.tile_pool(name="dists", bufs=1) as dists,
        tc.tile_pool(name="tables", bufs=1) as tables,
    ):
        def load_table(a):
            table = tables.tile([P, S], F32, name=f"table{a}")
            nc.sync.dma_start(table[:], emb[a * P:(a + 1) * P, :])
            return table

        counts = held.tile([2 * DF_AT, P], F32, name="counts")
        for row in (0, C):
            nc.sync.dma_start(counts[row:row + C, :], tf.rearrange("o (c p) -> (o c) p", p=P))
            nc.scalar.dma_start(counts[DF_AT + row:DF_AT + row + C, :], df.rearrange("o (c p) -> (o c) p", p=P))
        offsets = held.tile([P, N // 16], U16, name="offsets")
        nc.sync.dma_start(offsets[:], offs)
        table = load_table(0)

        ident_f = held.tile([P, P], F32, name="ident_f")
        make_identity(nc, ident_f[:])
        share = held.tile([P, P], F32, name="share")
        nc.vector.memset(share[:], 1.0 / PAIRS)
        minus_half = held.tile([P, HEADS], F32, name="minus_half")
        nc.vector.memset(minus_half[:], -0.5)
        one_bf = held.tile([P, 1], BF16, name="one_bf")
        nc.vector.memset(one_bf[:], 1.0)
        ident_bf = held.tile([P, P], BF16, name="ident_bf")
        nc.vector.tensor_copy(ident_bf[:], ident_f[:])

        gamma = held.tile([P, HEADS], F32, name="gamma")
        nc.sync.dma_start(gamma[:], bn_gamma.rearrange("h o -> (h o)").partition_broadcast(P))
        fcw = held.tile([P, HEADS, P], BF16, name="fcw")
        nc.sync.dma_start(fcw[:], fc_w.rearrange("(a k) m -> k a m", k=P))
        fcb = held.tile([P, 1], F32, name="fcb")
        nc.sync.dma_start(fcb[:], fc_b)

        keys = held.tile([P, HEADS * DOCS * T, KEYW], BF16, name="keys")
        dist = [[dists.tile([P, KEPT], F32, name=f"dist{a}{b}") for b in range(DOCS)] for a in range(HEADS)]
        sum_once = held.tile([P, HEADS * DOCS], F32, name="sum_once")
        sum_twice = held.tile([P, HEADS * DOCS], F32, name="sum_twice")
        sq = held.tile([P, HEADS * DOCS * T], F32, name="sq")
        sqcol = held.tile([P, HEADS * DOCS * T], F32, name="sqcol")
        gain, shift = {}, {}

        with (
            tc.tile_pool(name="weights", bufs=1) as weights,
            tc.tile_pool(name="work", bufs=4) as work,
            tc.tile_pool(name="rounded", bufs=HEADS * DOCS) as rounded,
            tc.psum_pool(name="ps_gram", bufs=5) as ps_gram,
            tc.psum_pool(name="ps_turn", bufs=2) as ps_turn,
            tc.psum_pool(name="ps_prep", bufs=1) as ps_prep,
        ):
            hsum_ps = ps_prep.tile([P, HEADS * DOCS * T], F32, name="hsum_ps")
            counts_ps = ps_gram.tile([P, 2 * DF_AT], F32, name="counts_ps", tag="gram_ps")
            nc.tensor.transpose(counts_ps[:], counts[:], ident_f[0:2 * DF_AT, 0:2 * DF_AT])
            ln_tf = held.tile([P, C], F32, name="ln_tf")
            ln_df = held.tile([P, C], F32, name="ln_df")
            nc.scalar.activation(ln_df[:], counts_ps[:, DF_AT:DF_AT + C], ACT.Ln, bias=2.0)
            nc.scalar.activation(ln_tf[:], counts_ps[:, 0:C], ACT.Ln, bias=1.0)
            inv_ln_df = held.tile([P, C], F32, name="inv_ln_df")
            nc.vector.reciprocal(inv_ln_df[:], ln_df[:])
            wt_c = held.tile([P, C], F32, name="wt_c")
            nc.vector.tensor_mul(wt_c[:], ln_tf[:], inv_ln_df[:])
            wt = [weights.tile([P, L], F32, name=f"wt{b}") for b in range(DOCS)]
            for b in range(DOCS):
                wt_ps = ps_gram.tile([P, L], F32, name="wt_ps", tag="gram_ps")
                for t in range(T):
                    c = b * T + t
                    nc.tensor.transpose(
                        wt_ps[:, t * P:(t + 1) * P], wt_c[:, c:c + 1].to_broadcast([P, P]), ident_f[:]
                    )
                nc.scalar.activation(wt[b][:], wt_ps[:], ACT.Copy)

            def look_up(a, b, table):
                block = (a * DOCS + b) * T
                h = work.tile([P, L], F32, name="h")
                nc.vector.tensor_tensor(
                    h[:],
                    table[:].indirect(offsets[:, b * (L // 16):(b + 1) * (L // 16)]),
                    wt[b][:],
                    ALU.mult,
                )
                hb = rounded.tile([P, L], BF16, name="hb")
                if b == DOCS - 1:
                    nc.scalar.copy(hb[:], h[:])
                else:
                    nc.vector.tensor_copy(hb[:], h[:])
                hT_ps = ps_turn.tile([P, T, P], F32, name="hT_ps")
                for t in range(T):
                    nc.tensor.transpose(hT_ps[:, t, :], h[:, t * P:(t + 1) * P], ident_f[:])
                for t in range(T):
                    squares = work.tile([P, P], F32, name="squares")
                    nc.scalar.activation(
                        squares[:], hT_ps[:, t, :], ACT.Square, accum_out=sq[:, block + t:block + t + 1]
                    )
                nc.scalar.activation(sqcol[:, block:block + T], sq[:, block:block + T], ACT.Copy, scale=-0.5)
                nc.scalar.activation(keys[:, block:block + T, 0:P], hT_ps[:], ACT.Copy)
                for t in range(T):
                    nc.tensor.matmul(
                        hsum_ps[:, block + t:block + t + 1], keys[:, block + t, 0:P], one_bf[:], start=True, stop=True
                    )
                return hb

            def distances(a, b, hb):
                block = (a * DOCS + b) * T
                for t in range(T):
                    gram_ps = ps_gram.tile([P, L], F32, name="gram_ps")
                    width = WIDTH[t]
                    nc.tensor.matmul(gram_ps[:, 0:width], hb[:, t * P:(t + 1) * P], hb[:, t * P:L], start=True, stop=False)
                    for s in range(t, T):
                        nc.tensor.matmul(
                            gram_ps[:, (s - t) * P:(s - t + 1) * P],
                            sqcol[:, block + s:block + s + 1].to_broadcast([P, P]), ident_f[:],
                            start=False, stop=(s == T - 1), is_transpose=True,
                        )
                    nc.vector.tensor_scalar(
                        row_block(dist[a][b], t), gram_ps[:, 0:width].rearrange("p (s c) -> p s c", c=P),
                        sqcol[:, block + t:block + t + 1], 0.0, ALU.add, ALU.min,
                    )
                unit = a * DOCS + b
                for (begin, width), sums in zip(RUNS, (sum_twice, sum_once)):
                    run = dist[a][b][:, begin:begin + width]
                    nc.scalar.activation(
                        run, run, ACT.Sqrt, scale=-2.0, bias=TINY, accum_out=sums[:, unit:unit + 1],
                    )

            def statistics(heads):
                first, count = heads[0], len(heads)

                def mine(columns, each):
                    return columns[:, first * each:(first + count) * each]

                def per_head(out, columns):
                    nc.vector.tensor_reduce(out, columns.rearrange("p (a c) -> p a c", a=count), AX.X, ALU.add)

                def column(name, width=count):
                    return held.tile([P, width], F32, name=f"{name}{first}")

                hsum, hsum_sq = column("hsum", count * DOCS), column("hsum_sq", count * DOCS)
                nc.vector.tensor_reduce(
                    hsum[:], mine(hsum_ps, DOCS * T).rearrange("p (c t) -> p c t", t=T), AX.X, ALU.add
                )
                nc.vector.tensor_mul(hsum_sq[:], hsum[:], hsum[:])
                sum_hsum_sq, sum_sqcol = column("sum_hsum_sq"), column("sum_sqcol")
                per_head(sum_hsum_sq[:], hsum_sq[:])
                per_head(sum_sqcol[:], mine(sqcol, DOCS * T))
                units_here = DOCS * count
                sums = column("sums", units_here + count)
                nc.vector.scalar_tensor_tensor(
                    sums[:, units_here:units_here + count], sum_sqcol[:], 2.0 * L, sum_hsum_sq[:], ALU.mult, ALU.add
                )
                nc.vector.scalar_tensor_tensor(
                    sums[:, 0:units_here], mine(sum_twice, DOCS), 2.0, mine(sum_once, DOCS), ALU.mult, ALU.add
                )
                mean_ps = ps_turn.tile([P, units_here + count], F32, name="mean_ps", tag="hT_ps")
                nc.tensor.matmul(mean_ps[:], share[:], sums[:], start=True, stop=True)
                mean, mean_sq_eps, sq_mean, var_eps = column("mean"), column("mean_sq_eps"), column("sq_mean"), column("var_eps")
                per_head(mean[:], mean_ps[:, 0:units_here])
                nc.vector.tensor_scalar(
                    mean_sq_eps[:], mean_ps[:, units_here:units_here + count], -2.0, TINY + EPS_BN, ALU.mult, ALU.add
                )
                nc.vector.tensor_mul(sq_mean[:], mean[:], mean[:])
                nc.vector.tensor_sub(var_eps[:], mean_sq_eps[:], sq_mean[:])
                inv_sd, gains, shifts = column("inv_sd"), column("gains"), column("shifts")
                nc.gpsimd.tensor_tensor(inv_sd[:], var_eps[:], minus_half[:, 0:count], ALU.pow)
                nc.vector.tensor_mul(gains[:], gamma[:, first:first + count], inv_sd[:])
                nc.vector.scalar_tensor_tensor(shifts[:], mean[:], -1.0, gains[:], ALU.mult, ALU.mult)
                for i, a in enumerate(heads):
                    gain[a], shift[a] = gains[:, i:i + 1], shifts[:, i:i + 1]

            units = [(a, b) for a in range(HEADS) for b in range(DOCS)]
            hb = {}
            for step in range(len(units) + LEAD):
                if step < len(units):
                    a, b = units[step]
                    if b == 0 and a > 0:
                        table = load_table(a)
                    hb[a, b] = look_up(a, b, table)
                if step == len(units):
                    statistics(range(HEADS - 1))
                if step >= LEAD:
                    a, b = units[step - LEAD]
                    distances(a, b, hb[a, b])
            statistics([HEADS - 1])

        received = held.tile([P, HEADS * DOCS * T], F32, name="received")
        with (
            tc.tile_pool(name="exps", bufs=4) as exps,
            tc.tile_pool(name="small", bufs=4) as small,
            tc.tile_pool(name="vos", bufs=4) as vos,
            tc.tile_pool(name="outs", bufs=2) as outs,
            tc.psum_pool(name="ps_v", bufs=3) as ps_v,
            tc.psum_pool(name="ps_e", bufs=2) as ps_e,
            tc.psum_pool(name="ps_t", bufs=2) as ps_t,
            tc.psum_pool(name="ps_o", bufs=1) as ps_o,
        ):
            def block_of(e, t, s):
                return e[:, t, s * P:(s + 1) * P]

            def exponentials(a, b):
                e = exps.tile([P, T, L], BF16, name="e")
                right_sum = small.tile([P, T], F32, name="right_sum")
                rowsum = small.tile([P, T], F32, name="rowsum")
                for t in range(T):
                    nc.scalar.activation(
                        e[:, t, FIRST[t]:L].rearrange("p (s c) -> p s c", c=P), row_block(dist[a][b], t), ACT.Exp,
                        bias=shift[a], scale=gain[a],
                        accum_out=(rowsum if t == 0 else right_sum)[:, t:t + 1],
                    )
                return e, right_sum, rowsum

            def mirror(a, b, e, right_sum, rowsum):
                block = (a * DOCS + b) * T
                eT_ps = ps_e.tile([P, MIRRORED], BF16, name="eT_ps")
                for t in range(1, T):
                    for s in range(t):
                        nc.tensor.transpose(
                            eT_ps[:, BELOW[t] + s * P:BELOW[t] + (s + 1) * P], block_of(e, s, t), ident_bf[:]
                        )
                for t in range(1, T):
                    nc.vector.tensor_scalar(
                        e[:, t, 0:FIRST[t]], eT_ps[:, BELOW[t]:BELOW[t] + FIRST[t]], 1.0, right_sum[:, t:t + 1],
                        ALU.mult, ALU.add, accum_out=rowsum[:, t:t + 1],
                    )
                rinv = small.tile([P, T], F32, name="rinv")
                nc.vector.reciprocal(rinv[:], rowsum[:])
                nc.vector.tensor_copy(keys[:, block:block + T, P:P + 1].squeeze(2), rinv[:])
                return rinv

            def weighted_sums(a, b, e, rinv):
                block = (a * DOCS + b) * T
                voT = small.tile([P, T, P], BF16, name="voT")
                for pair in range(T // 2):
                    v_ps = ps_v.tile([P, 2, BANK // 2], F32, name="v_ps")
                    for g in range(2):
                        s = 2 * pair + g
                        for t in range(T):
                            nc.tensor.matmul(
                                v_ps[:, g, 0:P + 1], block_of(e, t, s), keys[:, block + t, 0:P + 1],
                                start=(t == 0), stop=(t == T - 1),
                            )
                    nc.vector.tensor_tensor(
                        voT[:, 2 * pair:2 * pair + 2, :], v_ps[:, :, 0:P],
                        rinv[:, 2 * pair:2 * pair + 2].unsqueeze(2).to_broadcast([P, 2, P]), ALU.mult,
                    )
                    nc.vector.tensor_copy(
                        received[:, block + 2 * pair:block + 2 * pair + 2], v_ps[:, :, P:P + 1].squeeze(2)
                    )
                return voT

            def channels_first(voT):
                vo_ps = ps_t.tile([P, L], BF16, name="vo_ps")
                for s in range(T):
                    nc.tensor.transpose(vo_ps[:, s * P:(s + 1) * P], voT[:, s, :], ident_bf[:])
                vo_a = vos.tile([P, L], BF16, name="vo_a")
                nc.vector.tensor_copy(vo_a[:], vo_ps[:])
                return vo_a

            lg_ps = {}

            def class_scores(a, b, vo_a):
                if a == 0:
                    lg_ps[b] = ps_o.tile([P, L], F32, name="lg_ps")
                nc.tensor.matmul(lg_ps[b][:], fcw[:, a, :], vo_a[:], start=(a == 0), stop=(a == HEADS - 1))
                if a == HEADS - 1:
                    lg = outs.tile([P, L], F32, name="lg")
                    nc.vector.tensor_scalar_add(lg[:], lg_ps[b][:], fcb[:, 0:1])
                    nc.sync.dma_start(out[0:P, b * L:(b + 1) * L], lg[:])

            def last_row():
                received_sum = small.tile([P, DOCS * T], F32, name="received_sum")
                nc.vector.tensor_reduce(
                    received_sum[:], received[:].rearrange("p (a c) -> p c a", a=HEADS), AX.X, ALU.add
                )
                ws_ps = ps_t.tile([P, P], F32, name="ws_ps", tag="vo_ps")
                nc.tensor.transpose(ws_ps[0:DOCS * T, :], received_sum[:], ident_f[:])
                ws = outs.tile([DOCS * T, P], F32, name="ws")
                nc.vector.tensor_scalar_mul(ws[:], ws_ps[0:DOCS * T, :], 1.0 / HEADS)
                nc.sync.dma_start(out[P:P + 1, :].rearrange("o (c p) -> (o c) p", p=P), ws[:])

            units = [(a, b) for b in range(DOCS) for a in range(HEADS)]
            e_of, sums_of, rinv_of, voT_of, vo_of = {}, {}, {}, {}, {}
            for step in range(len(units) + 4):
                if step < len(units):
                    a, b = units[step]
                    e_of[step], *sums_of[step] = exponentials(a, b)
                if 0 <= step - 1 < len(units):
                    a, b = units[step - 1]
                    rinv_of[step - 1] = mirror(a, b, e_of[step - 1], *sums_of[step - 1])
                if 0 <= step - 2 < len(units):
                    a, b = units[step - 2]
                    voT_of[step - 2] = weighted_sums(a, b, e_of[step - 2], rinv_of[step - 2])
                if step - 2 == len(units) - 1:
                    last_row()
                if 0 <= step - 3 < len(units):
                    a, b = units[step - 3]
                    vo_of[step - 3] = channels_first(voT_of[step - 3])
                if 0 <= step - 4 < len(units):
                    a, b = units[step - 4]
                    class_scores(a, b, vo_of[step - 4])
